import numpy as np
import ml_dtypes


def mxq(x, axis, fmt="e4m3"):
    dtype, down = {"e4m3": (ml_dtypes.float8_e4m3fn, 7), "e5m2": (ml_dtypes.float8_e5m2, 14)}[fmt]
    v = np.moveaxis(np.asarray(x, np.float32).astype(ml_dtypes.bfloat16).astype(np.float64), axis, -1)
    blocks = v.reshape(v.shape[:-1] + (-1, 32))
    amax = np.abs(blocks).max(-1, keepdims=True)
    byte = np.maximum(np.where(amax > 0, np.frexp(amax)[1] - 1 + 127, 0) - down, 1)
    scale = np.exp2(byte - 127.0)
    codes = (blocks / scale).astype(np.float32).astype(dtype).astype(np.float64)
    return np.moveaxis((codes * scale).reshape(v.shape), -1, axis)


WIDE = False


def mx_kscale(k):
    if not WIDE:
        return np.ones(k)
    levels = np.array([10, -10, 5, -5, 0])
    if k % 512:
        return np.exp2(np.random.permutation(np.resize(levels, k // 32))).repeat(32)
    a = np.empty((k // 512, 16))
    for p in range(k // 512):
        a[p, :8] = np.random.permutation(np.resize(levels, 8))
        for g in range(8):
            far = levels[np.abs(levels - a[p, g]) >= 10]
            a[p, g + 8] = far[np.random.randint(len(far))]
    return np.exp2(a.ravel()).repeat(32)


BF16 = ml_dtypes.bfloat16


def bf(x):
    return np.asarray(x, np.float32).astype(BF16)


def f64(x):
    return np.asarray(x).astype(np.float64)


B, P, WS, D, H = 2, 24, 8, 1024, 16
WN = P // WS
N = WS * WS
SHIFT = WS // 2
LN_EPS = 1e-5


def layer_norm(x, g, b):
    mu = x.mean(-1, keepdims=True)
    var = x.var(-1, keepdims=True)
    return (x - mu) / np.sqrt(var + LN_EPS) * g + b


def window_merge(win):
    x = win.reshape(B, WN, WN, WS, WS, D).transpose(0, 1, 3, 2, 4, 5)
    return x.reshape(B, P, P, D)


def setup_inputs():
    s, t = mx_kscale(D), mx_kscale(D)
    x_mid = np.random.standard_normal((B, P * P, D)) * 1.4 + np.random.standard_normal((B, P * P, 1)) * 0.5
    return {"attn_win": bf(np.random.standard_normal((B * WN * WN, N, D)) * 0.4 * s),
            "x_mid": bf(x_mid),
            "Wo2": bf(np.random.standard_normal((D, D)) / np.sqrt(D) / s[:, None]),
            "bo2": bf(0.1 * np.random.standard_normal(D)),
            "g4": bf((1.0 + 0.1 * np.random.standard_normal(D)) * t),
            "b4": bf(0.1 * np.random.standard_normal(D) * t),
            "Wl": bf(np.random.standard_normal((D, D)) / np.sqrt(D) / t[:, None]),
            "bl": bf(0.1 * np.random.standard_normal(D))}


def reference(attn_win, x_mid, Wo2, bo2, g4, b4, Wl, bl):
    a = (mxq(f64(attn_win), 2, "e4m3") @ mxq(f64(Wo2), 0, "e4m3")) + f64(bo2)
    a = np.roll(window_merge(a), (-SHIFT, -SHIFT), axis=(1, 2)).reshape(B, P * P, D)
    x = f64(x_mid) + a
    h = layer_norm(x, f64(g4), f64(b4))
    return x + (mxq(h, 2, "e4m3") @ mxq(f64(Wl), 0, "e4m3")) + f64(bl)

@@ -1,0 +1,310 @@
+from contextlib import ExitStack
+
+import concourse.mybir as mybir
+from concourse.masks import make_identity
+
+F32 = mybir.dt.float32
+BF16 = mybir.dt.bfloat16
+U32 = mybir.dt.uint32
+U8 = mybir.dt.uint8
+FP8X4 = mybir.dt.float8_e4m3fn_x4
+ALU = mybir.AluOpType
+ACT = mybir.ActivationFunctionType
+
+P = 128
+D = 1024
+PACK = 4
+K_PASS = P * PACK
+PASSES = D // K_PASS
+N_PASS = 512
+HALVES = D // N_PASS
+IMAGES = 2
+SIDE = 24
+WS = 8
+WN = SIDE // WS
+SHIFT = WS // 2
+TOKENS = IMAGES * SIDE * SIDE
+TILES = TOKENS // P
+LN_EPS = 1e-5
+FLOPS = 2 * 2 * TOKENS * D * D
+
+
+def rolled_runs(w):
+    start = WS * w - SHIFT
+    if start < 0:
+        return [(0, SHIFT, start + SIDE), (SHIFT, WS - SHIFT, 0)]
+    return [(0, WS, start)]
+
+
+EARLY_ATTN = 5
+V_COLS = 320
+
+
+def quantise_weight(nc, stage, raw, codes, scales, g):
+    for h in range(HALVES):
+        first = h * N_PASS
+        grouped = stage.tile([P, N_PASS, PACK], BF16, align_bytes=64)
+        nc.vector.tensor_copy(
+            out=grouped[:, 0:V_COLS, :].rearrange("p (c i) t -> p c t i", i=4),
+            in_=raw[:, g * PACK : (g + 1) * PACK, first : first + V_COLS].rearrange("p t (c i) -> p c t i", i=4),
+        )
+        nc.scalar.copy(
+            out=grouped[:, V_COLS:N_PASS, :].rearrange("p (c i) t -> p c t i", i=4),
+            in_=raw[:, g * PACK : (g + 1) * PACK, first + V_COLS : first + N_PASS].rearrange(
+                "p t (c i) -> p c t i", i=4
+            ),
+        )
+        nc.vector.quantize_mx(
+            out=codes[:, g, first : first + N_PASS].bitcast(FP8X4),
+            scales=scales[:, g, first : first + N_PASS],
+            in_=grouped[:].rearrange("p n t -> p (n t)"),
+        )
+
+
+def tile_successiveswintransfomerblock_pb_kernel(tc, attn_win, x_mid, Wo2, bo2, g4, b4, Wl, bl, out):
+    nc = tc.nc
+    attn_rows = attn_win.flatten_outer_dims()
+    xmid_rows = x_mid.flatten_outer_dims()
+    out_rows = out.flatten_outer_dims()
+
+    with ExitStack() as ctx:
+        keep = ctx.enter_context(tc.tile_pool(name="keep", bufs=1))
+        stage = ctx.enter_context(tc.tile_pool(name="stage", bufs=3))
+        ahead = ctx.enter_context(tc.tile_pool(name="ahead", bufs=4))
+        rows_pool = ctx.enter_context(tc.tile_pool(name="rows_pool", bufs=8))
+        short = ctx.enter_context(tc.tile_pool(name="short", bufs=3))
+        small = ctx.enter_context(tc.tile_pool(name="small", bufs=8))
+        psum_acc1 = ctx.enter_context(tc.psum_pool(name="psum_acc1", bufs=2))
+        psum_acc2 = ctx.enter_context(tc.psum_pool(name="psum_acc2", bufs=4))
+        psum_tr = ctx.enter_context(tc.psum_pool(name="psum_tr", bufs=2))
+        ctx.enter_context(tc.manual_schedule())
+
+        gain_raw = keep.tile([P, PASSES, PACK], BF16)
+        shift_raw = keep.tile([P, PASSES, PACK], BF16)
+        bias_rows = keep.tile([P, 2 * D], BF16)
+        nc.vector.memset(bias_rows[:], 0.0)
+        nc.sync.dma_start(out=bias_rows[0:1, 0:D], in_=bo2.rearrange("(o d) -> o d", o=1))
+        nc.sync.dma_start(out=bias_rows[0:1, D : 2 * D], in_=bl.rearrange("(o d) -> o d", o=1))
+        ones = keep.tile([P, P], BF16)
+        nc.vector.memset(ones[:], 1.0)
+        eps = keep.tile([P, 1], F32)
+        nc.vector.memset(eps[:], LN_EPS)
+        ident = keep.tile([P, P], F32)
+        make_identity(nc, ident[:])
+
+        attn_sb = keep.tile([P, TILES, D], BF16)
+        attn_src = attn_rows.rearrange("(s q) d -> q s d", q=P)
+        xmid_sb = keep.tile([P, TILES, D], BF16)
+        xmid_src = xmid_rows.rearrange("(s q) d -> q s d", q=P)
+        wo_raw = keep.tile([P, PASSES * PACK, D], BF16)
+        wo_dst = wo_raw[:].rearrange("p (g t) n -> p g (t n)", t=PACK)
+        wo_src = Wo2.rearrange("(g p t) n -> p g (t n)", p=P, t=PACK)
+        wl_raw = keep.tile([P, PASSES * PACK, D], BF16)
+        wl_dst = wl_raw[:].rearrange("p (g t) n -> p g (t n)", t=PACK)
+        wl_src = Wl.rearrange("(g p t) n -> p g (t n)", p=P, t=PACK)
+
+        for g in range(PASSES):
+            nc.sync.dma_start(out=wo_dst[:, g, :], in_=wo_src[:, g, :])
+        nc.sync.dma_start(out=attn_sb[:, 0:3, :], in_=attn_src[:, 0:3, :])
+        nc.sync.dma_start(out=xmid_sb[:, 0:3, :], in_=xmid_src[:, 0:3, :])
+        nc.sync.dma_start(out=gain_raw[:], in_=g4.rearrange("(g p t) -> p g t", p=P, t=PACK))
+        nc.sync.dma_start(out=shift_raw[:], in_=b4.rearrange("(g p t) -> p g t", p=P, t=PACK))
+        for first in range(3, TILES, 3):
+            nc.sync.dma_start(out=attn_sb[:, first : first + 3, :], in_=attn_src[:, first : first + 3, :])
+        for g in range(PASSES):
+            nc.sync.dma_start(out=wl_dst[:, g, :], in_=wl_src[:, g, :])
+        for first in range(3, TILES, 3):
+            nc.sync.dma_start(out=xmid_sb[:, first : first + 3, :], in_=xmid_src[:, first : first + 3, :])
+
+        wo_codes = keep.tile([P, PASSES, D], U32, align_bytes=64)
+        wo_scales = keep.tile([P, PASSES, D], U8, align_bytes=64)
+        wl_codes = keep.tile([P, PASSES, D], U32, align_bytes=64)
+        wl_scales = keep.tile([P, PASSES, D], U8, align_bytes=64)
+        attn_grouped = keep.tile([P, PASSES, TOKENS, PACK], BF16, align_bytes=64)
+        attn_codes = keep.tile([P, PASSES, TOKENS], U32, align_bytes=64)
+        attn_scales = keep.tile([P, PASSES, TOKENS], U8, align_bytes=64)
+        by_patch = attn_grouped[:].bitcast(F32).rearrange("p g (b r c) u -> p g b r c u", r=SIDE, c=SIDE)
+
+        def flip_attn(s):
+            flipped = psum_acc2.tile([P, PASSES * 2, P], F32, tag="acc2")
+            for c in range(PASSES * 2):
+                g, u = divmod(c, 2)
+                words = attn_sb[:, s, :].bitcast(F32)[:, 2 * P * g + u : 2 * P * (g + 1) : 2]
+                nc.tensor.transpose(flipped[:, c, :], words, ident[:])
+            by_window = flipped[:].rearrange("p c (w i j) -> p c w i j", i=WS, j=WS)
+            for w in range(2):
+                image, in_image = divmod(2 * s + w, WN * WN)
+                wr, wc = divmod(in_image, WN)
+                for i0, n_rows, r0 in rolled_runs(wr):
+                    for j0, n_cols, c0 in rolled_runs(wc):
+                        for g in range(PASSES):
+                            src = by_window[:, 2 * g : 2 * g + 2, w, i0 : i0 + n_rows, j0 : j0 + n_cols]
+                            dst = by_patch[:, g, image, r0 : r0 + n_rows, c0 : c0 + n_cols, :]
+                            nc.scalar.copy(out=dst, in_=src.rearrange("p u i j -> p i j u"))
+
+        def quantise_attn(i):
+            toks = slice(i * P, (i + 1) * P)
+            for g in range(PASSES):
+                nc.vector.quantize_mx(
+                    out=attn_codes[:, g, toks].bitcast(FP8X4),
+                    scales=attn_scales[:, g, toks],
+                    in_=attn_grouped[:, g, toks, :].rearrange("p n t -> p (n t)"),
+                )
+
+        xb, acc1, x, negmean, rstd, shift, xn, flipped_xn, planes, h_codes, h_scales, acc2 = (
+            {}, {}, {}, {}, {}, {}, {}, {}, {}, {}, {}, {},
+        )
+
+        def add_bo2(i):
+            xb[i] = ahead.tile([P, D], F32, name="xb")
+            nc.gpsimd.tensor_tensor(out=xb[i][:], in0=xmid_sb[:, i, :], in1=bias_all[:, 0:D], op=ALU.add)
+
+        def project(i):
+            toks = slice(i * P, (i + 1) * P)
+            for h in range(HALVES):
+                cols = slice(h * N_PASS, (h + 1) * N_PASS)
+                acc1[i, h] = psum_acc1.tile([P, N_PASS], F32, name="acc1")
+                for g in range(PASSES):
+                    nc.tensor.matmul_mx(
+                        out=acc1[i, h][:],
+                        lhsT=attn_codes[:, g, toks].bitcast(FP8X4),
+                        lhsT_scale=attn_scales[:, g, toks],
+                        rhs=wo_codes[:, g, cols].bitcast(FP8X4),
+                        rhs_scale=wo_scales[:, g, cols],
+                        start=(g == 0),
+                        stop=(g == PASSES - 1),
+                    )
+
+        def residual(i):
+            x[i] = rows_pool.tile([P, D], F32, name="x")
+            sums = small.tile([P, HALVES], F32)
+            for h in range(HALVES):
+                cols = slice(h * N_PASS, (h + 1) * N_PASS)
+                nc.vector.scalar_tensor_tensor(
+                    out=x[i][:, cols], in0=acc1[i, h][:], scalar=1.0, in1=xb[i][:, cols],
+                    op0=ALU.mult, op1=ALU.add, accum_out=sums[:, h : h + 1],
+                )
+            negmean[i] = small.tile([P, 1], F32, name="negmean")
+            nc.vector.tensor_scalar(
+                out=negmean[i][:], in0=sums[:, 0:1], scalar1=sums[:, 1:2], scalar2=-1.0 / D,
+                op0=ALU.add, op1=ALU.mult,
+            )
+
+        def add_bl(i):
+            nc.gpsimd.tensor_tensor(out=x[i][:], in0=x[i][:], in1=bias_all[:, D : 2 * D], op=ALU.add)
+
+        def statistics(i):
+            squares = short.tile([P, D], BF16)
+            ssq = small.tile([P, 1], F32)
+            nc.scalar.activation(
+                out=squares[:], in_=x[i][:], func=ACT.Square, bias=negmean[i][:], scale=1.0, accum_out=ssq[:]
+            )
+            rstd[i] = small.tile([P, 1], F32, name="rstd")
+            nc.scalar.activation(out=rstd[i][:], in_=ssq[:], func=ACT.Abs_reciprocal_sqrt, bias=eps[:], scale=1.0 / D)
+            shift[i] = small.tile([P, 1], F32, name="shift")
+            nc.scalar.activation(out=shift[i][:], in_=negmean[i][:], func=ACT.Identity, scale=rstd[i][:])
+
+        def normalise(i):
+            xn[i] = short.tile([P, PASSES, PACK, P], F32, name="xn")
+            nc.scalar.activation(
+                out=xn[i][:].rearrange("p g t m -> p g m t"),
+                in_=x[i][:].rearrange("p (g m t) -> p g m t", g=PASSES, t=PACK), func=ACT.Identity,
+                bias=shift[i][:], scale=rstd[i][:],
+            )
+
+        def flip(i):
+            for g in range(PASSES):
+                flipped_xn[i, g] = psum_tr.tile([P, PACK, P], F32, name="flipped_xn", tag="tr")
+                for t in range(PACK):
+                    nc.tensor.transpose(flipped_xn[i, g][:, t, :], xn[i][:, g, t, :], ident[:])
+
+        def gain_and_bias(i):
+            planes[i] = short.tile([P, PASSES * PACK, P], BF16, name="planes")
+            for c in range(PASSES * PACK):
+                nc.scalar.activation(
+                    out=planes[i][:, c, :], in_=flipped_xn[i, c // PACK][:, c % PACK, :], func=ACT.Identity,
+                    bias=vec_cols[:, 8 + c : 9 + c], scale=vec_cols[:, c : c + 1],
+                )
+
+        def quantise_h(i):
+            h_grouped = short.tile([P, PASSES, P, PACK], BF16, align_bytes=64)
+            nc.vector.tensor_copy(out=h_grouped[:], in_=planes[i][:].rearrange("p (g t) n -> p g n t", t=PACK))
+            h_codes[i] = short.tile([P, PASSES, P], U32, align_bytes=64, name="h_codes")
+            h_scales[i] = short.tile([P, PASSES, P], U8, align_bytes=64, name="h_scales")
+            nc.vector.quantize_mx(
+                out=h_codes[i][:].rearrange("p g n -> p (g n)").bitcast(FP8X4),
+                scales=h_scales[i][:].rearrange("p g n -> p (g n)"),
+                in_=h_grouped[:].rearrange("p g n t -> p (g n t)"),
+            )
+
+        def linear(i):
+            for h in range(HALVES):
+                cols = slice(h * N_PASS, (h + 1) * N_PASS)
+                acc2[i, h] = psum_acc2.tile([P, N_PASS], F32, name="acc2")
+                for g in range(PASSES):
+                    nc.tensor.matmul_mx(
+                        out=acc2[i, h][:],
+                        lhsT=h_codes[i][:, g, :].bitcast(FP8X4),
+                        lhsT_scale=h_scales[i][:, g, :],
+                        rhs=wl_codes[:, g, cols].bitcast(FP8X4),
+                        rhs_scale=wl_scales[:, g, cols],
+                        start=(g == 0),
+                        stop=(g == PASSES - 1),
+                    )
+
+        def finish(i):
+            for h in range(HALVES):
+                cols = slice(h * N_PASS, (h + 1) * N_PASS)
+                nc.vector.tensor_tensor(out=x[i][:, cols], in0=acc2[i, h][:], in1=x[i][:, cols], op=ALU.add)
+            nc.sync.dma_start(out=out_rows[i * P : (i + 1) * P, :], in_=x[i][:])
+
+        bias_all = keep.tile([P, 2 * D], BF16)
+        for j in range(2 * HALVES):
+            cols = slice(j * N_PASS, (j + 1) * N_PASS)
+            spread = psum_tr.tile([P, N_PASS], F32, tag="tr")
+            nc.tensor.matmul(out=spread[:], lhsT=ones[:], rhs=bias_rows[:, cols], start=True, stop=True)
+            nc.scalar.copy(out=bias_all[:, cols], in_=spread[:])
+        vec_cols = keep.tile([P, 2 * PASSES * PACK], F32)
+
+        for g in range(PASSES):
+            quantise_weight(nc, stage, wo_raw, wo_codes, wo_scales, g)
+        for s in range(3):
+            flip_attn(s)
+        quantise_attn(0)
+        quantise_attn(1)
+        for i in range(3):
+            add_bo2(i)
+        project(0)
+        nc.vector.tensor_copy(out=vec_cols[:, 0:8], in_=gain_raw[:].rearrange("p g t -> p (g t)"))
+        nc.vector.tensor_copy(out=vec_cols[:, 8:16], in_=shift_raw[:].rearrange("p g t -> p (g t)"))
+        for s in range(3, EARLY_ATTN):
+            flip_attn(s)
+        quantise_attn(2)
+
+        for k in range(TILES + 5):
+            if 0 <= k - 2 < TILES:
+                flip(k - 2)
+            if 0 <= k - 1 < TILES:
+                statistics(k - 1)
+            if k < TILES:
+                residual(k)
+            if k < PASSES:
+                quantise_weight(nc, stage, wl_raw, wl_codes, wl_scales, k)
+            if 0 <= k - 1 < TILES:
+                normalise(k - 1)
+            if 0 <= k - 2 < TILES:
+                gain_and_bias(k - 2)
+                add_bl(k - 2)
+            if EARLY_ATTN + k < TILES:
+                flip_attn(EARLY_ATTN + k)
+            if 0 <= k - 4 < TILES:
+                finish(k - 4)
+            if 0 <= k - 3 < TILES:
+                linear(k - 3)
+            if k + 1 < TILES:
+                project(k + 1)
+            if 0 <= k - 2 < TILES:
+                quantise_h(k - 2)
+            if k + 3 < TILES:
+                quantise_attn(k + 3)
+                add_bo2(k + 3)

@@ -37,7 +37,7 @@ def rolled_runs(w):
 
 
 EARLY_ATTN = 5
-V_COLS = 320
+V_COLS = 128
 
 
 def quantise_weight(nc, stage, raw, codes, scales, g):
@@ -157,7 +157,7 @@ def tile_successiveswintransfomerblock_pb_kernel(tc, attn_win, x_mid, Wo2, bo2, 
 
         def add_bo2(i):
             xb[i] = ahead.tile([P, D], F32, name="xb")
-            nc.gpsimd.tensor_tensor(out=xb[i][:], in0=xmid_sb[:, i, :], in1=bias_all[:, 0:D], op=ALU.add)
+            nc.vector.tensor_tensor(out=xb[i][:], in0=xmid_sb[:, i, :], in1=bias_all[:, 0:D], op=ALU.add)
 
         def project(i):
             toks = slice(i * P, (i + 1) * P)
@@ -191,7 +191,7 @@ def tile_successiveswintransfomerblock_pb_kernel(tc, attn_win, x_mid, Wo2, bo2, 
             )
 
         def add_bl(i):
-            nc.gpsimd.tensor_tensor(out=x[i][:], in0=x[i][:], in1=bias_all[:, D : 2 * D], op=ALU.add)
+            nc.vector.tensor_tensor(out=x[i][:], in0=x[i][:], in1=bias_all[:, D : 2 * D], op=ALU.add)
 
         def statistics(i):
             squares = short.tile([P, D], BF16)
@@ -272,8 +272,7 @@ def tile_successiveswintransfomerblock_pb_kernel(tc, attn_win, x_mid, Wo2, bo2, 
             flip_attn(s)
         quantise_attn(0)
         quantise_attn(1)
-        for i in range(3):
-            add_bo2(i)
+        add_bo2(0)
         project(0)
         nc.vector.tensor_copy(out=vec_cols[:, 0:8], in_=gain_raw[:].rearrange("p g t -> p (g t)"))
         nc.vector.tensor_copy(out=vec_cols[:, 8:16], in_=shift_raw[:].rearrange("p g t -> p (g t)"))
@@ -299,6 +298,8 @@ def tile_successiveswintransfomerblock_pb_kernel(tc, attn_win, x_mid, Wo2, bo2, 
                 flip_attn(EARLY_ATTN + k)
             if 0 <= k - 4 < TILES:
                 finish(k - 4)
+            if k + 1 < TILES:
+                add_bo2(k + 1)
             if 0 <= k - 3 < TILES:
                 linear(k - 3)
             if k + 1 < TILES:
@@ -307,4 +308,3 @@ def tile_successiveswintransfomerblock_pb_kernel(tc, attn_win, x_mid, Wo2, bo2, 
                 quantise_h(k - 2)
             if k + 3 < TILES:
                 quantise_attn(k + 3)
-                add_bo2(k + 3)

@@ -28,37 +28,17 @@ TILES = TOKENS // P
 LN_EPS = 1e-5
 FLOPS = 2 * 2 * TOKENS * D * D
 
+EARLY_ATTN = 5
+EARLY_XB = 3
+V_COLS_WO = 320
+V_COLS_WL = 192
+
 
 def rolled_runs(w):
     start = WS * w - SHIFT
     if start < 0:
         return [(0, SHIFT, start + SIDE), (SHIFT, WS - SHIFT, 0)]
     return [(0, WS, start)]
-
-
-EARLY_ATTN = 5
-V_COLS = 128
-
-
-def quantise_weight(nc, stage, raw, codes, scales, g):
-    for h in range(HALVES):
-        first = h * N_PASS
-        grouped = stage.tile([P, N_PASS, PACK], BF16, align_bytes=64)
-        nc.vector.tensor_copy(
-            out=grouped[:, 0:V_COLS, :].rearrange("p (c i) t -> p c t i", i=4),
-            in_=raw[:, g * PACK : (g + 1) * PACK, first : first + V_COLS].rearrange("p t (c i) -> p c t i", i=4),
-        )
-        nc.scalar.copy(
-            out=grouped[:, V_COLS:N_PASS, :].rearrange("p (c i) t -> p c t i", i=4),
-            in_=raw[:, g * PACK : (g + 1) * PACK, first + V_COLS : first + N_PASS].rearrange(
-                "p t (c i) -> p c t i", i=4
-            ),
-        )
-        nc.vector.quantize_mx(
-            out=codes[:, g, first : first + N_PASS].bitcast(FP8X4),
-            scales=scales[:, g, first : first + N_PASS],
-            in_=grouped[:].rearrange("p n t -> p (n t)"),
-        )
 
 
 def tile_successiveswintransfomerblock_pb_kernel(tc, attn_win, x_mid, Wo2, bo2, g4, b4, Wl, bl, out):
@@ -69,52 +49,67 @@ def tile_successiveswintransfomerblock_pb_kernel(tc, attn_win, x_mid, Wo2, bo2, 
 
     with ExitStack() as ctx:
         keep = ctx.enter_context(tc.tile_pool(name="keep", bufs=1))
-        stage = ctx.enter_context(tc.tile_pool(name="stage", bufs=3))
+        stage = ctx.enter_context(tc.tile_pool(name="stage", bufs=4))
         ahead = ctx.enter_context(tc.tile_pool(name="ahead", bufs=4))
-        rows_pool = ctx.enter_context(tc.tile_pool(name="rows_pool", bufs=8))
+        rows_pool = ctx.enter_context(tc.tile_pool(name="rows_pool", bufs=7))
         short = ctx.enter_context(tc.tile_pool(name="short", bufs=3))
         small = ctx.enter_context(tc.tile_pool(name="small", bufs=8))
         psum_acc1 = ctx.enter_context(tc.psum_pool(name="psum_acc1", bufs=2))
-        psum_acc2 = ctx.enter_context(tc.psum_pool(name="psum_acc2", bufs=4))
+        psum_mix = ctx.enter_context(tc.psum_pool(name="psum_mix", bufs=4))
         psum_tr = ctx.enter_context(tc.psum_pool(name="psum_tr", bufs=2))
         ctx.enter_context(tc.manual_schedule())
 
-        gain_raw = keep.tile([P, PASSES, PACK], BF16)
-        shift_raw = keep.tile([P, PASSES, PACK], BF16)
-        bias_rows = keep.tile([P, 2 * D], BF16)
-        nc.vector.memset(bias_rows[:], 0.0)
-        nc.sync.dma_start(out=bias_rows[0:1, 0:D], in_=bo2.rearrange("(o d) -> o d", o=1))
-        nc.sync.dma_start(out=bias_rows[0:1, D : 2 * D], in_=bl.rearrange("(o d) -> o d", o=1))
         ones = keep.tile([P, P], BF16)
         nc.vector.memset(ones[:], 1.0)
         eps = keep.tile([P, 1], F32)
         nc.vector.memset(eps[:], LN_EPS)
+        warm = keep.tile([P, 1], F32)
+        nc.scalar.activation(out=warm[:], in_=eps[:], func=ACT.Abs_reciprocal_sqrt)
+        bias_rows = keep.tile([P, 2 * D], BF16)
+        nc.vector.memset(bias_rows[:].bitcast(F32), 0.0)
+        gain_raw = keep.tile([P, PASSES, PACK], BF16)
+        shift_raw = keep.tile([P, PASSES, PACK], BF16)
+        nc.scalar.dma_start(out=bias_rows[0:1, 0:D], in_=bo2.rearrange("(o d) -> o d", o=1))
+        nc.scalar.dma_start(out=bias_rows[0:1, D : 2 * D], in_=bl.rearrange("(o d) -> o d", o=1))
+        nc.scalar.dma_start(out=gain_raw[:], in_=g4.rearrange("(g p t) -> p g t", p=P, t=PACK))
+        nc.scalar.dma_start(out=shift_raw[:], in_=b4.rearrange("(g p t) -> p g t", p=P, t=PACK))
         ident = keep.tile([P, P], F32)
         make_identity(nc, ident[:])
+        ident_bf = keep.tile([P, P], BF16)
+        nc.gpsimd.tensor_copy(out=ident_bf[:], in_=ident[:])
+        bias_all = keep.tile([P, 2 * D], BF16)
+        vec_cols = keep.tile([P, 2 * PASSES * PACK], F32)
 
         attn_sb = keep.tile([P, TILES, D], BF16)
         attn_src = attn_rows.rearrange("(s q) d -> q s d", q=P)
         xmid_sb = keep.tile([P, TILES, D], BF16)
         xmid_src = xmid_rows.rearrange("(s q) d -> q s d", q=P)
-        wo_raw = keep.tile([P, PASSES * PACK, D], BF16)
-        wo_dst = wo_raw[:].rearrange("p (g t) n -> p g (t n)", t=PACK)
-        wo_src = Wo2.rearrange("(g p t) n -> p g (t n)", p=P, t=PACK)
-        wl_raw = keep.tile([P, PASSES * PACK, D], BF16)
-        wl_dst = wl_raw[:].rearrange("p (g t) n -> p g (t n)", t=PACK)
-        wl_src = Wl.rearrange("(g p t) n -> p g (t n)", p=P, t=PACK)
+        wo_src = Wo2.rearrange("(g p t) n -> p g t n", p=P, t=PACK)
+        wl_src = Wl.rearrange("(g p t) n -> p g t n", p=P, t=PACK)
+        raw = {}
 
-        for g in range(PASSES):
-            nc.sync.dma_start(out=wo_dst[:, g, :], in_=wo_src[:, g, :])
-        nc.sync.dma_start(out=attn_sb[:, 0:3, :], in_=attn_src[:, 0:3, :])
-        nc.sync.dma_start(out=xmid_sb[:, 0:3, :], in_=xmid_src[:, 0:3, :])
-        nc.sync.dma_start(out=gain_raw[:], in_=g4.rearrange("(g p t) -> p g t", p=P, t=PACK))
-        nc.sync.dma_start(out=shift_raw[:], in_=b4.rearrange("(g p t) -> p g t", p=P, t=PACK))
-        for first in range(3, TILES, 3):
-            nc.sync.dma_start(out=attn_sb[:, first : first + 3, :], in_=attn_src[:, first : first + 3, :])
-        for g in range(PASSES):
-            nc.sync.dma_start(out=wl_dst[:, g, :], in_=wl_src[:, g, :])
-        for first in range(3, TILES, 3):
-            nc.sync.dma_start(out=xmid_sb[:, first : first + 3, :], in_=xmid_src[:, first : first + 3, :])
+        def load_weight(name, src, g, h):
+            raw[name, g, h] = keep.tile([P, PACK, N_PASS], BF16, name="raw", tag="raw_%s_%d%d" % (name, g, h))
+            nc.sync.dma_start(out=raw[name, g, h][:], in_=src[:, g, :, h * N_PASS : (h + 1) * N_PASS])
+
+        def load_rows(dst, src, first, last):
+            nc.sync.dma_start(out=dst[:, first:last, :], in_=src[:, first:last, :])
+
+        load_rows(attn_sb, attn_src, 0, 1)
+        for h in range(HALVES):
+            for g in range(PASSES):
+                load_weight("wo", wo_src, g, h)
+            if h == 0:
+                load_rows(attn_sb, attn_src, 1, 3)
+                load_rows(xmid_sb, xmid_src, 0, 1)
+        load_rows(xmid_sb, xmid_src, 1, 3)
+        load_rows(attn_sb, attn_src, 3, 6)
+        for h in range(HALVES):
+            for g in range(PASSES):
+                load_weight("wl", wl_src, g, h)
+        load_rows(xmid_sb, xmid_src, 3, 6)
+        load_rows(attn_sb, attn_src, 6, 9)
+        load_rows(xmid_sb, xmid_src, 6, 9)
 
         wo_codes = keep.tile([P, PASSES, D], U32, align_bytes=64)
         wo_scales = keep.tile([P, PASSES, D], U8, align_bytes=64)
@@ -125,13 +120,36 @@ def tile_successiveswintransfomerblock_pb_kernel(tc, attn_win, x_mid, Wo2, bo2, 
         attn_scales = keep.tile([P, PASSES, TOKENS], U8, align_bytes=64)
         by_patch = attn_grouped[:].bitcast(F32).rearrange("p g (b r c) u -> p g b r c u", r=SIDE, c=SIDE)
 
+        grouped = {}
+
+        def regroup(name, v_cols, g, h):
+            grouped[name, g, h] = stage.tile([P, N_PASS, PACK], BF16, align_bytes=64, name="grouped")
+            dst = grouped[name, g, h]
+            src = raw[name, g, h]
+            for engine_copy, cols in ((nc.vector.tensor_copy, slice(0, v_cols)), (nc.scalar.copy, slice(v_cols, N_PASS))):
+                engine_copy(
+                    out=dst[:, cols, :].rearrange("p (c i) t -> p c t i", i=4),
+                    in_=src[:, :, cols].rearrange("p t (c i) -> p c t i", i=4),
+                )
+
+        def quantise_weight(codes, scales, name, g, h):
+            cols = slice(h * N_PASS, (h + 1) * N_PASS)
+            nc.vector.quantize_mx(
+                out=codes[:, g, cols].bitcast(FP8X4), scales=scales[:, g, cols],
+                in_=grouped[name, g, h][:].rearrange("p n t -> p (n t)"),
+            )
+
+        flipped_attn = {}
+
         def flip_attn(s):
-            flipped = psum_acc2.tile([P, PASSES * 2, P], F32, tag="acc2")
+            flipped_attn[s] = psum_mix.tile([P, PASSES * 2, P], F32, name="flipped_attn", tag="mix")
             for c in range(PASSES * 2):
                 g, u = divmod(c, 2)
                 words = attn_sb[:, s, :].bitcast(F32)[:, 2 * P * g + u : 2 * P * (g + 1) : 2]
-                nc.tensor.transpose(flipped[:, c, :], words, ident[:])
-            by_window = flipped[:].rearrange("p c (w i j) -> p c w i j", i=WS, j=WS)
+                nc.tensor.transpose(flipped_attn[s][:, c, :], words, ident[:])
+
+        def place_attn(s):
+            by_window = flipped_attn[s][:].rearrange("p c (w i j) -> p c w i j", i=WS, j=WS)
             for w in range(2):
                 image, in_image = divmod(2 * s + w, WN * WN)
                 wr, wc = divmod(in_image, WN)
@@ -151,13 +169,25 @@ def tile_successiveswintransfomerblock_pb_kernel(tc, attn_win, x_mid, Wo2, bo2, 
                     in_=attn_grouped[:, g, toks, :].rearrange("p n t -> p (n t)"),
                 )
 
-        xb, acc1, x, negmean, rstd, shift, xn, flipped_xn, planes, h_codes, h_scales, acc2 = (
-            {}, {}, {}, {}, {}, {}, {}, {}, {}, {}, {}, {},
+        xb, xb_ps, acc1, x, sums, negmean, ssq, rstd, shift, xn, flipped_xn, planes, h_grouped, h_codes, h_scales, acc2 = (
+            {}, {}, {}, {}, {}, {}, {}, {}, {}, {}, {}, {}, {}, {}, {}, {},
         )
 
-        def add_bo2(i):
+        def xb_on_vector(i):
             xb[i] = ahead.tile([P, D], F32, name="xb")
             nc.vector.tensor_tensor(out=xb[i][:], in0=xmid_sb[:, i, :], in1=bias_all[:, 0:D], op=ALU.add)
+
+        def xb_on_tensor(i):
+            for h in range(HALVES):
+                cols = slice(h * N_PASS, (h + 1) * N_PASS)
+                xb_ps[i, h] = psum_mix.tile([P, N_PASS], F32, name="xb_ps", tag="mix")
+                nc.tensor.matmul(out=xb_ps[i, h][:], lhsT=ones[:], rhs=bias_rows[:, cols], start=True, stop=False)
+                nc.tensor.matmul(out=xb_ps[i, h][:], lhsT=ident_bf[:], rhs=xmid_sb[:, i, cols], start=False, stop=True)
+
+        def xb_copy(i):
+            xb[i] = ahead.tile([P, D], F32, name="xb")
+            for h in range(HALVES):
+                nc.scalar.copy(out=xb[i][:, h * N_PASS : (h + 1) * N_PASS], in_=xb_ps[i, h][:])
 
         def project(i):
             toks = slice(i * P, (i + 1) * P)
@@ -177,70 +207,87 @@ def tile_successiveswintransfomerblock_pb_kernel(tc, attn_win, x_mid, Wo2, bo2, 
 
         def residual(i):
             x[i] = rows_pool.tile([P, D], F32, name="x")
-            sums = small.tile([P, HALVES], F32)
+            sums[i] = small.tile([P, HALVES], F32, name="sums")
             for h in range(HALVES):
                 cols = slice(h * N_PASS, (h + 1) * N_PASS)
                 nc.vector.scalar_tensor_tensor(
                     out=x[i][:, cols], in0=acc1[i, h][:], scalar=1.0, in1=xb[i][:, cols],
-                    op0=ALU.mult, op1=ALU.add, accum_out=sums[:, h : h + 1],
+                    op0=ALU.mult, op1=ALU.add, accum_out=sums[i][:, h : h + 1],
                 )
+
+        def mean(i):
             negmean[i] = small.tile([P, 1], F32, name="negmean")
             nc.vector.tensor_scalar(
-                out=negmean[i][:], in0=sums[:, 0:1], scalar1=sums[:, 1:2], scalar2=-1.0 / D,
+                out=negmean[i][:], in0=sums[i][:, 0:1], scalar1=sums[i][:, 1:2], scalar2=-1.0 / D,
                 op0=ALU.add, op1=ALU.mult,
             )
 
         def add_bl(i):
             nc.vector.tensor_tensor(out=x[i][:], in0=x[i][:], in1=bias_all[:, D : 2 * D], op=ALU.add)
 
-        def statistics(i):
+        def square(i):
             squares = short.tile([P, D], BF16)
-            ssq = small.tile([P, 1], F32)
+            ssq[i] = small.tile([P, 1], F32, name="ssq")
             nc.scalar.activation(
-                out=squares[:], in_=x[i][:], func=ACT.Square, bias=negmean[i][:], scale=1.0, accum_out=ssq[:]
+                out=squares[:], in_=x[i][:], func=ACT.Square, bias=negmean[i][:], scale=1.0, accum_out=ssq[i][:]
             )
+
+        def scale_of(i):
             rstd[i] = small.tile([P, 1], F32, name="rstd")
-            nc.scalar.activation(out=rstd[i][:], in_=ssq[:], func=ACT.Abs_reciprocal_sqrt, bias=eps[:], scale=1.0 / D)
+            nc.scalar.activation(out=rstd[i][:], in_=ssq[i][:], func=ACT.Abs_reciprocal_sqrt, bias=eps[:], scale=1.0 / D)
+
+        def shift_of(i):
             shift[i] = small.tile([P, 1], F32, name="shift")
             nc.scalar.activation(out=shift[i][:], in_=negmean[i][:], func=ACT.Identity, scale=rstd[i][:])
 
         def normalise(i):
-            xn[i] = short.tile([P, PASSES, PACK, P], F32, name="xn")
-            nc.scalar.activation(
-                out=xn[i][:].rearrange("p g t m -> p g m t"),
-                in_=x[i][:].rearrange("p (g m t) -> p g m t", g=PASSES, t=PACK), func=ACT.Identity,
-                bias=shift[i][:], scale=rstd[i][:],
-            )
+            for g in range(PASSES):
+                xn[i, g] = short.tile([P, PACK, P], F32, name="xn", tag="xn%d" % g)
+                nc.scalar.activation(
+                    out=xn[i, g][:].rearrange("p t m -> p m t"),
+                    in_=x[i][:, g * K_PASS : (g + 1) * K_PASS].rearrange("p (m t) -> p m t", t=PACK),
+                    func=ACT.Identity, bias=shift[i][:], scale=rstd[i][:],
+                )
 
         def flip(i):
             for g in range(PASSES):
                 flipped_xn[i, g] = psum_tr.tile([P, PACK, P], F32, name="flipped_xn", tag="tr")
                 for t in range(PACK):
-                    nc.tensor.transpose(flipped_xn[i, g][:, t, :], xn[i][:, g, t, :], ident[:])
+                    nc.tensor.transpose(flipped_xn[i, g][:, t, :], xn[i, g][:, t, :], ident[:])
 
-        def gain_and_bias(i):
-            planes[i] = short.tile([P, PASSES * PACK, P], BF16, name="planes")
-            for c in range(PASSES * PACK):
-                nc.scalar.activation(
-                    out=planes[i][:, c, :], in_=flipped_xn[i, c // PACK][:, c % PACK, :], func=ACT.Identity,
-                    bias=vec_cols[:, 8 + c : 9 + c], scale=vec_cols[:, c : c + 1],
-                )
+        def gain_and_bias(i, g, on_vector=False):
+            planes[i, g] = short.tile([P, PACK, P], BF16, name="planes", tag="planes%d" % g)
+            for t in range(PACK):
+                c = g * PACK + t
+                gain, bias = vec_cols[:, c : c + 1], vec_cols[:, 8 + c : 9 + c]
+                if on_vector:
+                    nc.vector.tensor_scalar(
+                        out=planes[i, g][:, t, :], in0=flipped_xn[i, g][:, t, :], scalar1=gain, scalar2=bias,
+                        op0=ALU.mult, op1=ALU.add,
+                    )
+                else:
+                    nc.scalar.activation(
+                        out=planes[i, g][:, t, :], in_=flipped_xn[i, g][:, t, :], func=ACT.Identity, bias=bias, scale=gain
+                    )
+
+        def regroup_h(i):
+            for g in range(PASSES):
+                h_grouped[i, g] = short.tile([P, P, PACK], BF16, align_bytes=64, name="h_grouped", tag="h_grouped%d" % g)
+                nc.vector.tensor_copy(out=h_grouped[i, g][:], in_=planes[i, g][:].rearrange("p t n -> p n t"))
 
         def quantise_h(i):
-            h_grouped = short.tile([P, PASSES, P, PACK], BF16, align_bytes=64)
-            nc.vector.tensor_copy(out=h_grouped[:], in_=planes[i][:].rearrange("p (g t) n -> p g n t", t=PACK))
             h_codes[i] = short.tile([P, PASSES, P], U32, align_bytes=64, name="h_codes")
             h_scales[i] = short.tile([P, PASSES, P], U8, align_bytes=64, name="h_scales")
-            nc.vector.quantize_mx(
-                out=h_codes[i][:].rearrange("p g n -> p (g n)").bitcast(FP8X4),
-                scales=h_scales[i][:].rearrange("p g n -> p (g n)"),
-                in_=h_grouped[:].rearrange("p g n t -> p (g n t)"),
-            )
+            for g in range(PASSES):
+                nc.vector.quantize_mx(
+                    out=h_codes[i][:, g, :].bitcast(FP8X4), scales=h_scales[i][:, g, :],
+                    in_=h_grouped[i, g][:].rearrange("p n t -> p (n t)"),
+                )
 
         def linear(i):
             for h in range(HALVES):
                 cols = slice(h * N_PASS, (h + 1) * N_PASS)
-                acc2[i, h] = psum_acc2.tile([P, N_PASS], F32, name="acc2")
+                acc2[i, h] = psum_mix.tile([P, N_PASS], F32, name="acc2", tag="mix")
                 for g in range(PASSES):
                     nc.tensor.matmul_mx(
                         out=acc2[i, h][:],
@@ -256,55 +303,87 @@ def tile_successiveswintransfomerblock_pb_kernel(tc, attn_win, x_mid, Wo2, bo2, 
             for h in range(HALVES):
                 cols = slice(h * N_PASS, (h + 1) * N_PASS)
                 nc.vector.tensor_tensor(out=x[i][:, cols], in0=acc2[i, h][:], in1=x[i][:, cols], op=ALU.add)
-            nc.sync.dma_start(out=out_rows[i * P : (i + 1) * P, :], in_=x[i][:])
+                nc.sync.dma_start(out=out_rows[i * P : (i + 1) * P, cols], in_=x[i][:, cols])
 
-        bias_all = keep.tile([P, 2 * D], BF16)
-        for j in range(2 * HALVES):
+        def spread(j):
             cols = slice(j * N_PASS, (j + 1) * N_PASS)
-            spread = psum_tr.tile([P, N_PASS], F32, tag="tr")
-            nc.tensor.matmul(out=spread[:], lhsT=ones[:], rhs=bias_rows[:, cols], start=True, stop=True)
-            nc.scalar.copy(out=bias_all[:, cols], in_=spread[:])
-        vec_cols = keep.tile([P, 2 * PASSES * PACK], F32)
+            spread_ps = psum_tr.tile([P, N_PASS], F32, name="spread_ps", tag="tr")
+            nc.tensor.matmul(out=spread_ps[:], lhsT=ones[:], rhs=bias_rows[:, cols], start=True, stop=True)
+            nc.scalar.copy(out=bias_all[:, cols], in_=spread_ps[:])
 
-        for g in range(PASSES):
-            quantise_weight(nc, stage, wo_raw, wo_codes, wo_scales, g)
-        for s in range(3):
-            flip_attn(s)
+        spread(0)
+        spread(1)
+        flip_attn(0)
+        place_attn(0)
+        regroup("wo", V_COLS_WO, 0, 0)
+        regroup("wo", V_COLS_WO, 1, 0)
+        quantise_weight(wo_codes, wo_scales, "wo", 0, 0)
+        flip_attn(1)
+        flip_attn(2)
+        place_attn(1)
+        regroup("wo", V_COLS_WO, 0, 1)
+        quantise_weight(wo_codes, wo_scales, "wo", 1, 0)
+        place_attn(2)
+        regroup("wo", V_COLS_WO, 1, 1)
+        quantise_weight(wo_codes, wo_scales, "wo", 0, 1)
         quantise_attn(0)
-        quantise_attn(1)
-        add_bo2(0)
+        quantise_weight(wo_codes, wo_scales, "wo", 1, 1)
         project(0)
+        xb_on_vector(0)
+        quantise_attn(1)
         nc.vector.tensor_copy(out=vec_cols[:, 0:8], in_=gain_raw[:].rearrange("p g t -> p (g t)"))
         nc.vector.tensor_copy(out=vec_cols[:, 8:16], in_=shift_raw[:].rearrange("p g t -> p (g t)"))
+        spread(2)
+        spread(3)
         for s in range(3, EARLY_ATTN):
             flip_attn(s)
-        quantise_attn(2)
+            place_attn(s)
 
+        last = TILES - 1
         for k in range(TILES + 5):
-            if 0 <= k - 2 < TILES:
-                flip(k - 2)
-            if 0 <= k - 1 < TILES:
-                statistics(k - 1)
-            if k < TILES:
-                residual(k)
-            if k < PASSES:
-                quantise_weight(nc, stage, wl_raw, wl_codes, wl_scales, k)
-            if 0 <= k - 1 < TILES:
-                normalise(k - 1)
-            if 0 <= k - 2 < TILES:
-                gain_and_bias(k - 2)
-                add_bl(k - 2)
-            if EARLY_ATTN + k < TILES:
-                flip_attn(EARLY_ATTN + k)
-            if 0 <= k - 4 < TILES:
-                finish(k - 4)
-            if k + 1 < TILES:
-                add_bo2(k + 1)
-            if 0 <= k - 3 < TILES:
-                linear(k - 3)
+            a, b, c, e, f = k, k - 1, k - 2, k - 3, k - 4
+            if 0 <= c < TILES:
+                flip(c)
+            if 0 <= b < TILES:
+                square(b)
+            if a < TILES:
+                residual(a)
+            if 0 <= c < TILES:
+                gain_and_bias(c, 0)
+            if 0 <= b < TILES:
+                scale_of(b)
+            if 0 <= c < TILES:
+                gain_and_bias(c, 1, on_vector=(c == last))
+            if 0 <= b < TILES:
+                shift_of(b)
+            if k + 2 < TILES:
+                quantise_attn(k + 2)
+            if a < TILES:
+                mean(a)
             if k + 1 < TILES:
                 project(k + 1)
-            if 0 <= k - 2 < TILES:
-                quantise_h(k - 2)
-            if k + 3 < TILES:
-                quantise_attn(k + 3)
+            if k < HALVES:
+                for g in range(PASSES):
+                    regroup("wl", V_COLS_WL, g, k)
+            if EARLY_ATTN + k < TILES:
+                flip_attn(EARLY_ATTN + k)
+                place_attn(EARLY_ATTN + k)
+            if 0 <= b < TILES:
+                normalise(b)
+            if k < HALVES:
+                for g in range(PASSES):
+                    quantise_weight(wl_codes, wl_scales, "wl", g, k)
+            if k + 1 < EARLY_XB:
+                xb_on_vector(k + 1)
+            if EARLY_XB <= k + 2 < TILES:
+                xb_on_tensor(k + 2)
+                xb_copy(k + 2)
+            if 0 <= c < TILES:
+                add_bl(c)
+            if 0 <= f < TILES:
+                finish(f)
+            if 0 <= e < TILES:
+                linear(e)
+            if 0 <= c < TILES:
+                regroup_h(c)
+                quantise_h(c)

@@ -29,9 +29,11 @@ LN_EPS = 1e-5
 FLOPS = 2 * 2 * TOKENS * D * D
 
 EARLY_ATTN = 5
+XB_PE = (3, 4, 5, 6, 7, 8)
 EARLY_XB = 3
 V_COLS_WO = 320
-V_COLS_WL = 192
+V_COLS_WL = 320
+NORM_V = tuple(range(TILES))
 
 
 def rolled_runs(w):
@@ -55,7 +57,8 @@ def tile_successiveswintransfomerblock_pb_kernel(tc, attn_win, x_mid, Wo2, bo2, 
         short = ctx.enter_context(tc.tile_pool(name="short", bufs=3))
         small = ctx.enter_context(tc.tile_pool(name="small", bufs=8))
         psum_acc1 = ctx.enter_context(tc.psum_pool(name="psum_acc1", bufs=2))
-        psum_mix = ctx.enter_context(tc.psum_pool(name="psum_mix", bufs=4))
+        psum_mix = ctx.enter_context(tc.psum_pool(name="psum_mix", bufs=2))
+        psum_acc2 = ctx.enter_context(tc.psum_pool(name="psum_acc2", bufs=2))
         psum_tr = ctx.enter_context(tc.psum_pool(name="psum_tr", bufs=2))
         ctx.enter_context(tc.manual_schedule())
 
@@ -95,14 +98,13 @@ def tile_successiveswintransfomerblock_pb_kernel(tc, attn_win, x_mid, Wo2, bo2, 
         def load_rows(dst, src, first, last):
             nc.sync.dma_start(out=dst[:, first:last, :], in_=src[:, first:last, :])
 
-        load_rows(attn_sb, attn_src, 0, 1)
         for h in range(HALVES):
             for g in range(PASSES):
                 load_weight("wo", wo_src, g, h)
-            if h == 0:
-                load_rows(attn_sb, attn_src, 1, 3)
-                load_rows(xmid_sb, xmid_src, 0, 1)
-        load_rows(xmid_sb, xmid_src, 1, 3)
+                if h == 0 and g == 0:
+                    load_rows(attn_sb, attn_src, 0, 1)
+        load_rows(attn_sb, attn_src, 1, 3)
+        load_rows(xmid_sb, xmid_src, 0, 3)
         load_rows(attn_sb, attn_src, 3, 6)
         for h in range(HALVES):
             for g in range(PASSES):
@@ -223,7 +225,16 @@ def tile_successiveswintransfomerblock_pb_kernel(tc, attn_win, x_mid, Wo2, bo2, 
             )
 
         def add_bl(i):
-            nc.vector.tensor_tensor(out=x[i][:], in0=x[i][:], in1=bias_all[:, D : 2 * D], op=ALU.add)
+            for h in range(HALVES):
+                cols = slice(h * N_PASS, (h + 1) * N_PASS)
+                nc.vector.tensor_tensor(
+                    out=x[i][:, cols], in0=x[i][:, cols], in1=bias_all[:, D + h * N_PASS : D + (h + 1) * N_PASS], op=ALU.add
+                )
+
+        def add_bl_later(i):
+            tick = small.tile([P, 1], F32)
+            nc.gpsimd.tensor_copy(out=tick[:], in_=xn[i + 1, PASSES - 1][:, PACK - 1, P - 1 : P])
+            nc.gpsimd.tensor_tensor(out=x[i][:], in0=x[i][:], in1=bias_all[:, D : 2 * D], op=ALU.add)
 
         def square(i):
             squares = short.tile([P, D], BF16)
@@ -243,11 +254,14 @@ def tile_successiveswintransfomerblock_pb_kernel(tc, attn_win, x_mid, Wo2, bo2, 
         def normalise(i):
             for g in range(PASSES):
                 xn[i, g] = short.tile([P, PACK, P], F32, name="xn", tag="xn%d" % g)
-                nc.scalar.activation(
-                    out=xn[i, g][:].rearrange("p t m -> p m t"),
-                    in_=x[i][:, g * K_PASS : (g + 1) * K_PASS].rearrange("p (m t) -> p m t", t=PACK),
-                    func=ACT.Identity, bias=shift[i][:], scale=rstd[i][:],
-                )
+                dst = xn[i, g][:].rearrange("p t m -> p m t")
+                src = x[i][:, g * K_PASS : (g + 1) * K_PASS].rearrange("p (m t) -> p m t", t=PACK)
+                if i in NORM_V:
+                    nc.vector.tensor_scalar(
+                        out=dst, in0=src, scalar1=negmean[i][:], scalar2=rstd[i][:], op0=ALU.add, op1=ALU.mult
+                    )
+                else:
+                    nc.scalar.activation(out=dst, in_=src, func=ACT.Identity, bias=shift[i][:], scale=rstd[i][:])
 
         def flip(i):
             for g in range(PASSES):
@@ -287,7 +301,7 @@ def tile_successiveswintransfomerblock_pb_kernel(tc, attn_win, x_mid, Wo2, bo2, 
         def linear(i):
             for h in range(HALVES):
                 cols = slice(h * N_PASS, (h + 1) * N_PASS)
-                acc2[i, h] = psum_mix.tile([P, N_PASS], F32, name="acc2", tag="mix")
+                acc2[i, h] = psum_acc2.tile([P, N_PASS], F32, name="acc2")
                 for g in range(PASSES):
                     nc.tensor.matmul_mx(
                         out=acc2[i, h][:],
@@ -305,85 +319,101 @@ def tile_successiveswintransfomerblock_pb_kernel(tc, attn_win, x_mid, Wo2, bo2, 
                 nc.vector.tensor_tensor(out=x[i][:, cols], in0=acc2[i, h][:], in1=x[i][:, cols], op=ALU.add)
                 nc.sync.dma_start(out=out_rows[i * P : (i + 1) * P, cols], in_=x[i][:, cols])
 
+        spread_ps = {}
+
         def spread(j):
             cols = slice(j * N_PASS, (j + 1) * N_PASS)
-            spread_ps = psum_tr.tile([P, N_PASS], F32, name="spread_ps", tag="tr")
-            nc.tensor.matmul(out=spread_ps[:], lhsT=ones[:], rhs=bias_rows[:, cols], start=True, stop=True)
-            nc.scalar.copy(out=bias_all[:, cols], in_=spread_ps[:])
+            spread_ps[j] = psum_tr.tile([P, N_PASS], F32, name="spread_ps", tag="tr")
+            nc.tensor.matmul(out=spread_ps[j][:], lhsT=ones[:], rhs=bias_rows[:, cols], start=True, stop=True)
 
+        def spread_copy(j):
+            nc.scalar.copy(out=bias_all[:, j * N_PASS : (j + 1) * N_PASS], in_=spread_ps[j][:])
+
+        flip_attn(0)
         spread(0)
         spread(1)
-        flip_attn(0)
-        place_attn(0)
         regroup("wo", V_COLS_WO, 0, 0)
         regroup("wo", V_COLS_WO, 1, 0)
         quantise_weight(wo_codes, wo_scales, "wo", 0, 0)
+        spread_copy(0)
+        spread_copy(1)
+        regroup("wo", V_COLS_WO, 0, 1)
+        quantise_weight(wo_codes, wo_scales, "wo", 1, 0)
+        regroup("wo", V_COLS_WO, 1, 1)
+        quantise_weight(wo_codes, wo_scales, "wo", 0, 1)
+        place_attn(0)
         flip_attn(1)
         flip_attn(2)
         place_attn(1)
-        regroup("wo", V_COLS_WO, 0, 1)
-        quantise_weight(wo_codes, wo_scales, "wo", 1, 0)
-        place_attn(2)
-        regroup("wo", V_COLS_WO, 1, 1)
-        quantise_weight(wo_codes, wo_scales, "wo", 0, 1)
-        quantise_attn(0)
         quantise_weight(wo_codes, wo_scales, "wo", 1, 1)
-        project(0)
+        place_attn(2)
         xb_on_vector(0)
-        quantise_attn(1)
+        quantise_attn(0)
+        project(0)
+        xb_on_vector(1)
         nc.vector.tensor_copy(out=vec_cols[:, 0:8], in_=gain_raw[:].rearrange("p g t -> p (g t)"))
         nc.vector.tensor_copy(out=vec_cols[:, 8:16], in_=shift_raw[:].rearrange("p g t -> p (g t)"))
-        spread(2)
-        spread(3)
         for s in range(3, EARLY_ATTN):
             flip_attn(s)
             place_attn(s)
+        residual(0)
+        quantise_attn(1)
+        mean(0)
+        quantise_attn(2)
 
-        last = TILES - 1
-        for k in range(TILES + 5):
-            a, b, c, e, f = k, k - 1, k - 2, k - 3, k - 4
-            if 0 <= c < TILES:
-                flip(c)
-            if 0 <= b < TILES:
-                square(b)
-            if a < TILES:
-                residual(a)
-            if 0 <= c < TILES:
-                gain_and_bias(c, 0)
-            if 0 <= b < TILES:
-                scale_of(b)
-            if 0 <= c < TILES:
-                gain_and_bias(c, 1, on_vector=(c == last))
-            if 0 <= b < TILES:
-                shift_of(b)
-            if k + 2 < TILES:
-                quantise_attn(k + 2)
-            if a < TILES:
-                mean(a)
+        for k in range(TILES + 2):
+            if k + 2 in XB_PE:
+                xb_on_tensor(k + 2)
             if k + 1 < TILES:
                 project(k + 1)
-            if k < HALVES:
-                for g in range(PASSES):
-                    regroup("wl", V_COLS_WL, g, k)
+            if 3 <= k + 2 < TILES:
+                quantise_attn(k + 2)
+            if k < TILES:
+                square(k)
+                scale_of(k)
+            if k == 1:
+                quantise_weight(wl_codes, wl_scales, "wl", 1, 0)
+            if k + 2 in XB_PE:
+                xb_copy(k + 2)
+            elif 2 <= k + 2 < TILES:
+                xb_on_vector(k + 2)
             if EARLY_ATTN + k < TILES:
                 flip_attn(EARLY_ATTN + k)
                 place_attn(EARLY_ATTN + k)
-            if 0 <= b < TILES:
-                normalise(b)
+            if 0 < k <= TILES:
+                regroup_h(k - 1)
+                quantise_h(k - 1)
+            if k < TILES:
+                normalise(k)
+                flip(k)
             if k < HALVES:
-                for g in range(PASSES):
-                    quantise_weight(wl_codes, wl_scales, "wl", g, k)
-            if k + 1 < EARLY_XB:
-                xb_on_vector(k + 1)
-            if EARLY_XB <= k + 2 < TILES:
-                xb_on_tensor(k + 2)
-                xb_copy(k + 2)
-            if 0 <= c < TILES:
-                add_bl(c)
-            if 0 <= f < TILES:
-                finish(f)
-            if 0 <= e < TILES:
-                linear(e)
-            if 0 <= c < TILES:
-                regroup_h(c)
-                quantise_h(c)
+                regroup("wl", V_COLS_WL, 0, k)
+            if 0 < k <= TILES:
+                if k - 1 < TILES - 2:
+                    add_bl_later(k - 1)
+                elif k - 1 < TILES:
+                    add_bl(k - 1)
+            if 0 <= k - 2 < TILES - 1:
+                finish(k - 2)
+            if 1 < k <= TILES:
+                linear(k - 1)
+            if k + 1 < TILES:
+                residual(k + 1)
+                mean(k + 1)
+            if k < HALVES:
+                quantise_weight(wl_codes, wl_scales, "wl", 0, k)
+            if k < TILES:
+                gain_and_bias(k, 0)
+                gain_and_bias(k, 1, on_vector=(k == TILES - 1))
+            if k < HALVES:
+                regroup("wl", V_COLS_WL, 1, k)
+            if k == 0:
+                spread(2)
+                spread(3)
+                spread_copy(2)
+                spread_copy(3)
+            if k == 1:
+                quantise_weight(wl_codes, wl_scales, "wl", 1, 1)
+                linear(0)
+            if k == TILES:
+                finish(k - 1)

@@ -70,18 +70,18 @@ def tile_successiveswintransfomerblock_pb_kernel(tc, attn_win, x_mid, Wo2, bo2, 
         nc.scalar.activation(out=warm[:], in_=eps[:], func=ACT.Abs_reciprocal_sqrt)
         bias_rows = keep.tile([P, 2 * D], BF16)
         nc.vector.memset(bias_rows[:].bitcast(F32), 0.0)
-        gain_raw = keep.tile([P, PASSES, PACK], BF16)
-        shift_raw = keep.tile([P, PASSES, PACK], BF16)
+        vec_rows = keep.tile([P, K_PASS], BF16)
+        nc.gpsimd.memset(vec_rows[:].bitcast(F32), 0.0)
         nc.scalar.dma_start(out=bias_rows[0:1, 0:D], in_=bo2.rearrange("(o d) -> o d", o=1))
         nc.scalar.dma_start(out=bias_rows[0:1, D : 2 * D], in_=bl.rearrange("(o d) -> o d", o=1))
-        nc.scalar.dma_start(out=gain_raw[:], in_=g4.rearrange("(g p t) -> p g t", p=P, t=PACK))
-        nc.scalar.dma_start(out=shift_raw[:], in_=b4.rearrange("(g p t) -> p g t", p=P, t=PACK))
+        nc.scalar.dma_start(out=vec_rows[0:PASSES, :], in_=g4.rearrange("(g k) -> g k", g=PASSES))
+        nc.scalar.dma_start(out=vec_rows[PASSES : 2 * PASSES, :], in_=b4.rearrange("(g k) -> g k", g=PASSES))
         ident = keep.tile([P, P], F32)
         make_identity(nc, ident[:])
         ident_bf = keep.tile([P, P], BF16)
         nc.gpsimd.tensor_copy(out=ident_bf[:], in_=ident[:])
         bias_all = keep.tile([P, 2 * D], BF16)
-        vec_cols = keep.tile([P, 2 * PASSES * PACK], F32)
+        vec_cols = keep.tile([P, PACK, 2 * PASSES], F32)
 
         attn_sb = keep.tile([P, TILES, D], BF16)
         attn_src = attn_rows.rearrange("(s q) d -> q s d", q=P)
@@ -91,24 +91,22 @@ def tile_successiveswintransfomerblock_pb_kernel(tc, attn_win, x_mid, Wo2, bo2, 
         wl_src = Wl.rearrange("(g p t) n -> p g t n", p=P, t=PACK)
         raw = {}
 
-        def load_weight(name, src, g, h):
-            raw[name, g, h] = keep.tile([P, PACK, N_PASS], BF16, name="raw", tag="raw_%s_%d%d" % (name, g, h))
-            nc.sync.dma_start(out=raw[name, g, h][:], in_=src[:, g, :, h * N_PASS : (h + 1) * N_PASS])
+        def load_weight(name, src, g):
+            raw[name, g] = keep.tile([P, PACK, D], BF16, name="raw", tag="raw_%s_%d" % (name, g))
+            nc.sync.dma_start(out=raw[name, g][:], in_=src[:, g, :, :])
 
         def load_rows(dst, src, first, last):
             nc.sync.dma_start(out=dst[:, first:last, :], in_=src[:, first:last, :])
 
-        for h in range(HALVES):
-            for g in range(PASSES):
-                load_weight("wo", wo_src, g, h)
-                if h == 0 and g == 0:
-                    load_rows(attn_sb, attn_src, 0, 1)
+        for g in range(PASSES):
+            load_weight("wo", wo_src, g)
+            if g == 0:
+                load_rows(attn_sb, attn_src, 0, 1)
         load_rows(attn_sb, attn_src, 1, 3)
         load_rows(xmid_sb, xmid_src, 0, 3)
         load_rows(attn_sb, attn_src, 3, 6)
-        for h in range(HALVES):
-            for g in range(PASSES):
-                load_weight("wl", wl_src, g, h)
+        for g in range(PASSES):
+            load_weight("wl", wl_src, g)
         load_rows(xmid_sb, xmid_src, 3, 6)
         load_rows(attn_sb, attn_src, 6, 9)
         load_rows(xmid_sb, xmid_src, 6, 9)
@@ -127,7 +125,7 @@ def tile_successiveswintransfomerblock_pb_kernel(tc, attn_win, x_mid, Wo2, bo2, 
         def regroup(name, v_cols, g, h):
             grouped[name, g, h] = stage.tile([P, N_PASS, PACK], BF16, align_bytes=64, name="grouped")
             dst = grouped[name, g, h]
-            src = raw[name, g, h]
+            src = raw[name, g][:, :, h * N_PASS : (h + 1) * N_PASS]
             for engine_copy, cols in ((nc.vector.tensor_copy, slice(0, v_cols)), (nc.scalar.copy, slice(v_cols, N_PASS))):
                 engine_copy(
                     out=dst[:, cols, :].rearrange("p (c i) t -> p c t i", i=4),
@@ -195,7 +193,7 @@ def tile_successiveswintransfomerblock_pb_kernel(tc, attn_win, x_mid, Wo2, bo2, 
             toks = slice(i * P, (i + 1) * P)
             for h in range(HALVES):
                 cols = slice(h * N_PASS, (h + 1) * N_PASS)
-                acc1[i, h] = psum_acc1.tile([P, N_PASS], F32, name="acc1")
+                acc1[i, h] = psum_acc1.tile([P, N_PASS], F32, name="acc1", tag="acc1")
                 for g in range(PASSES):
                     nc.tensor.matmul_mx(
                         out=acc1[i, h][:],
@@ -272,8 +270,7 @@ def tile_successiveswintransfomerblock_pb_kernel(tc, attn_win, x_mid, Wo2, bo2, 
         def gain_and_bias(i, g, on_vector=False):
             planes[i, g] = short.tile([P, PACK, P], BF16, name="planes", tag="planes%d" % g)
             for t in range(PACK):
-                c = g * PACK + t
-                gain, bias = vec_cols[:, c : c + 1], vec_cols[:, 8 + c : 9 + c]
+                gain, bias = vec_cols[:, t, g : g + 1], vec_cols[:, t, PASSES + g : PASSES + g + 1]
                 if on_vector:
                     nc.vector.tensor_scalar(
                         out=planes[i, g][:, t, :], in0=flipped_xn[i, g][:, t, :], scalar1=gain, scalar2=bias,
@@ -333,26 +330,30 @@ def tile_successiveswintransfomerblock_pb_kernel(tc, attn_win, x_mid, Wo2, bo2, 
         spread(0)
         spread(1)
         regroup("wo", V_COLS_WO, 0, 0)
-        regroup("wo", V_COLS_WO, 1, 0)
+        regroup("wo", V_COLS_WO, 0, 1)
         quantise_weight(wo_codes, wo_scales, "wo", 0, 0)
         spread_copy(0)
         spread_copy(1)
-        regroup("wo", V_COLS_WO, 0, 1)
-        quantise_weight(wo_codes, wo_scales, "wo", 1, 0)
-        regroup("wo", V_COLS_WO, 1, 1)
+        regroup("wo", V_COLS_WO, 1, 0)
         quantise_weight(wo_codes, wo_scales, "wo", 0, 1)
+        regroup("wo", V_COLS_WO, 1, 1)
+        quantise_weight(wo_codes, wo_scales, "wo", 1, 0)
         place_attn(0)
         flip_attn(1)
         flip_attn(2)
         place_attn(1)
         quantise_weight(wo_codes, wo_scales, "wo", 1, 1)
         place_attn(2)
+        vec_f32 = keep.tile([P, K_PASS], F32)
+        nc.vector.tensor_copy(out=vec_f32[:], in_=vec_rows[:])
+        vec_ps = psum_acc1.tile([P, PACK, P], F32, name="vec_ps", tag="acc1")
+        for t in range(PACK):
+            nc.tensor.transpose(vec_ps[:, t, :], vec_f32[:, t::PACK], ident[:])
         xb_on_vector(0)
+        nc.vector.tensor_copy(out=vec_cols[:], in_=vec_ps[:, :, 0 : 2 * PASSES])
         quantise_attn(0)
         project(0)
         xb_on_vector(1)
-        nc.vector.tensor_copy(out=vec_cols[:, 0:8], in_=gain_raw[:].rearrange("p g t -> p (g t)"))
-        nc.vector.tensor_copy(out=vec_cols[:, 8:16], in_=shift_raw[:].rearrange("p g t -> p (g t)"))
         for s in range(3, EARLY_ATTN):
             flip_attn(s)
             place_attn(s)

@@ -30,6 +30,7 @@ FLOPS = 2 * 2 * TOKENS * D * D
 
 EARLY_ATTN = 5
 XB_PE = (3, 4, 5, 6, 7, 8)
+BL_V = (0, 6)
 EARLY_XB = 3
 V_COLS_WO = 320
 V_COLS_WL = 320
@@ -103,12 +104,12 @@ def tile_successiveswintransfomerblock_pb_kernel(tc, attn_win, x_mid, Wo2, bo2, 
             if g == 0:
                 load_rows(attn_sb, attn_src, 0, 1)
         load_rows(attn_sb, attn_src, 1, 3)
+        load_rows(attn_sb, attn_src, 3, 5)
         load_rows(xmid_sb, xmid_src, 0, 3)
-        load_rows(attn_sb, attn_src, 3, 6)
         for g in range(PASSES):
             load_weight("wl", wl_src, g)
+        load_rows(attn_sb, attn_src, 5, 9)
         load_rows(xmid_sb, xmid_src, 3, 6)
-        load_rows(attn_sb, attn_src, 6, 9)
         load_rows(xmid_sb, xmid_src, 6, 9)
 
         wo_codes = keep.tile([P, PASSES, D], U32, align_bytes=64)
@@ -142,7 +143,8 @@ def tile_successiveswintransfomerblock_pb_kernel(tc, attn_win, x_mid, Wo2, bo2, 
         flipped_attn = {}
 
         def flip_attn(s):
-            flipped_attn[s] = psum_mix.tile([P, PASSES * 2, P], F32, name="flipped_attn", tag="mix")
+            pool, tag = (psum_acc2, "acc2") if s in (1, 2, 4, 6, 7) else (psum_mix, "mix")
+            flipped_attn[s] = pool.tile([P, PASSES * 2, P], F32, name="flipped_attn", tag=tag)
             for c in range(PASSES * 2):
                 g, u = divmod(c, 2)
                 words = attn_sb[:, s, :].bitcast(F32)[:, 2 * P * g + u : 2 * P * (g + 1) : 2]
@@ -229,9 +231,9 @@ def tile_successiveswintransfomerblock_pb_kernel(tc, attn_win, x_mid, Wo2, bo2, 
                     out=x[i][:, cols], in0=x[i][:, cols], in1=bias_all[:, D + h * N_PASS : D + (h + 1) * N_PASS], op=ALU.add
                 )
 
-        def add_bl_later(i):
-            tick = small.tile([P, 1], F32)
-            nc.gpsimd.tensor_copy(out=tick[:], in_=xn[i + 1, PASSES - 1][:, PACK - 1, P - 1 : P])
+        def add_bl_later(i, dtype, last_written):
+            tick = small.tile([P, 1], dtype, name="tick", tag="tick")
+            nc.gpsimd.tensor_copy(out=tick[:], in_=last_written)
             nc.gpsimd.tensor_tensor(out=x[i][:], in0=x[i][:], in1=bias_all[:, D : 2 * D], op=ALU.add)
 
         def square(i):
@@ -298,7 +300,8 @@ def tile_successiveswintransfomerblock_pb_kernel(tc, attn_win, x_mid, Wo2, bo2, 
         def linear(i):
             for h in range(HALVES):
                 cols = slice(h * N_PASS, (h + 1) * N_PASS)
-                acc2[i, h] = psum_acc2.tile([P, N_PASS], F32, name="acc2")
+                pool, tag = {TILES - 2: (psum_mix, "mix"), TILES - 1: (psum_acc1, "acc1")}.get(i, (psum_acc2, "acc2"))
+                acc2[i, h] = pool.tile([P, N_PASS], F32, name="acc2", tag=tag)
                 for g in range(PASSES):
                     nc.tensor.matmul_mx(
                         out=acc2[i, h][:],
@@ -327,94 +330,109 @@ def tile_successiveswintransfomerblock_pb_kernel(tc, attn_win, x_mid, Wo2, bo2, 
             nc.scalar.copy(out=bias_all[:, j * N_PASS : (j + 1) * N_PASS], in_=spread_ps[j][:])
 
         flip_attn(0)
-        spread(0)
-        spread(1)
-        regroup("wo", V_COLS_WO, 0, 0)
-        regroup("wo", V_COLS_WO, 0, 1)
-        quantise_weight(wo_codes, wo_scales, "wo", 0, 0)
-        spread_copy(0)
-        spread_copy(1)
-        regroup("wo", V_COLS_WO, 1, 0)
-        quantise_weight(wo_codes, wo_scales, "wo", 0, 1)
-        regroup("wo", V_COLS_WO, 1, 1)
-        quantise_weight(wo_codes, wo_scales, "wo", 1, 0)
-        place_attn(0)
-        flip_attn(1)
-        flip_attn(2)
-        place_attn(1)
-        quantise_weight(wo_codes, wo_scales, "wo", 1, 1)
-        place_attn(2)
         vec_f32 = keep.tile([P, K_PASS], F32)
         nc.vector.tensor_copy(out=vec_f32[:], in_=vec_rows[:])
         vec_ps = psum_acc1.tile([P, PACK, P], F32, name="vec_ps", tag="acc1")
         for t in range(PACK):
             nc.tensor.transpose(vec_ps[:, t, :], vec_f32[:, t::PACK], ident[:])
-        xb_on_vector(0)
+        spread(0)
+        spread(1)
+        regroup("wo", V_COLS_WO, 0, 0)
+        regroup("wo", V_COLS_WO, 0, 1)
+        place_attn(0)
+        quantise_weight(wo_codes, wo_scales, "wo", 0, 0)
+        regroup("wo", V_COLS_WO, 1, 0)
+        quantise_weight(wo_codes, wo_scales, "wo", 0, 1)
         nc.vector.tensor_copy(out=vec_cols[:], in_=vec_ps[:, :, 0 : 2 * PASSES])
+        regroup("wo", V_COLS_WO, 1, 1)
+        quantise_weight(wo_codes, wo_scales, "wo", 1, 0)
+        flip_attn(1)
+        flip_attn(2)
+        place_attn(1)
+        quantise_weight(wo_codes, wo_scales, "wo", 1, 1)
+        place_attn(2)
         quantise_attn(0)
         project(0)
-        xb_on_vector(1)
+        spread_copy(0)
+        spread_copy(1)
+        xb_on_vector(0)
         for s in range(3, EARLY_ATTN):
             flip_attn(s)
             place_attn(s)
-        residual(0)
+        spread(2)
+        spread(3)
+        spread_copy(2)
+        spread_copy(3)
+        xb_on_vector(1)
         quantise_attn(1)
+        residual(0)
         mean(0)
+        project(1)
         quantise_attn(2)
+        square(0)
+        scale_of(0)
+        xb_on_vector(2)
+        flip_attn(5)
+        place_attn(5)
+        residual(1)
+        mean(1)
+        project(2)
+        square(1)
+        scale_of(1)
 
-        for k in range(TILES + 2):
-            if k + 2 in XB_PE:
-                xb_on_tensor(k + 2)
-            if k + 1 < TILES:
-                project(k + 1)
-            if 3 <= k + 2 < TILES:
-                quantise_attn(k + 2)
-            if k < TILES:
-                square(k)
-                scale_of(k)
-            if k == 1:
-                quantise_weight(wl_codes, wl_scales, "wl", 1, 0)
-            if k + 2 in XB_PE:
-                xb_copy(k + 2)
-            elif 2 <= k + 2 < TILES:
-                xb_on_vector(k + 2)
-            if EARLY_ATTN + k < TILES:
-                flip_attn(EARLY_ATTN + k)
-                place_attn(EARLY_ATTN + k)
-            if 0 < k <= TILES:
-                regroup_h(k - 1)
-                quantise_h(k - 1)
-            if k < TILES:
+        last = TILES - 1
+        for k in range(TILES):
+            if k < last:
                 normalise(k)
                 flip(k)
-            if k < HALVES:
-                regroup("wl", V_COLS_WL, 0, k)
-            if 0 < k <= TILES:
-                if k - 1 < TILES - 2:
-                    add_bl_later(k - 1)
-                elif k - 1 < TILES:
-                    add_bl(k - 1)
-            if 0 <= k - 2 < TILES - 1:
-                finish(k - 2)
-            if 1 < k <= TILES:
-                linear(k - 1)
-            if k + 1 < TILES:
-                residual(k + 1)
-                mean(k + 1)
-            if k < HALVES:
-                quantise_weight(wl_codes, wl_scales, "wl", 0, k)
-            if k < TILES:
+            if k == last - 1:
+                normalise(last)
                 gain_and_bias(k, 0)
-                gain_and_bias(k, 1, on_vector=(k == TILES - 1))
+                gain_and_bias(k, 1)
+                flip(last)
+            if k - 1 in BL_V:
+                add_bl(k - 1)
+            elif 0 < k < last:
+                add_bl_later(k - 1, F32, xn[k, PASSES - 1][:, PACK - 1, P - 1 : P])
+            if 1 < k < last:
+                finish(k - 2)
+                linear(k - 1)
+            if k + 3 in XB_PE:
+                xb_on_tensor(k + 3)
+            if k + 2 < TILES:
+                residual(k + 2)
+            if k + 3 < TILES:
+                quantise_attn(k + 3)
+            if k + 2 < TILES:
+                mean(k + 2)
             if k < HALVES:
-                regroup("wl", V_COLS_WL, 1, k)
-            if k == 0:
-                spread(2)
-                spread(3)
-                spread_copy(2)
-                spread_copy(3)
+                for g in range(PASSES):
+                    regroup("wl", V_COLS_WL, g, k)
+            if k != last - 1:
+                gain_and_bias(k, 0)
+                gain_and_bias(k, 1)
+            if k + 2 < TILES:
+                square(k + 2)
+                scale_of(k + 2)
+            if k + 3 < TILES:
+                project(k + 3)
+            if k + 3 in XB_PE:
+                xb_copy(k + 3)
+            if 6 + k < TILES:
+                flip_attn(6 + k)
+                place_attn(6 + k)
+            if k < HALVES:
+                for g in range(PASSES):
+                    quantise_weight(wl_codes, wl_scales, "wl", g, k)
+            regroup_h(k)
+            quantise_h(k)
+            if k == last - 1:
+                linear(k)
+                add_bl(k)
             if k == 1:
-                quantise_weight(wl_codes, wl_scales, "wl", 1, 1)
                 linear(0)
-            if k == TILES:
-                finish(k - 1)
+        add_bl_later(last, U32, h_codes[last][:, PASSES - 1, P - 1 : P])
+        linear(last)
+        finish(last - 2)
+        finish(last - 1)
+        finish(last)

@@ -30,6 +30,7 @@ FLOPS = 2 * 2 * TOKENS * D * D
 
 EARLY_ATTN = 5
 XB_PE = (3, 4, 5, 6, 7, 8)
+LATE_ATTN = {0: (6, 7), 2: (8,)}
 BL_V = (0, 6)
 EARLY_XB = 3
 V_COLS_WO = 320
@@ -330,11 +331,6 @@ def tile_successiveswintransfomerblock_pb_kernel(tc, attn_win, x_mid, Wo2, bo2, 
             nc.scalar.copy(out=bias_all[:, j * N_PASS : (j + 1) * N_PASS], in_=spread_ps[j][:])
 
         flip_attn(0)
-        vec_f32 = keep.tile([P, K_PASS], F32)
-        nc.vector.tensor_copy(out=vec_f32[:], in_=vec_rows[:])
-        vec_ps = psum_acc1.tile([P, PACK, P], F32, name="vec_ps", tag="acc1")
-        for t in range(PACK):
-            nc.tensor.transpose(vec_ps[:, t, :], vec_f32[:, t::PACK], ident[:])
         spread(0)
         spread(1)
         regroup("wo", V_COLS_WO, 0, 0)
@@ -343,7 +339,6 @@ def tile_successiveswintransfomerblock_pb_kernel(tc, attn_win, x_mid, Wo2, bo2, 
         quantise_weight(wo_codes, wo_scales, "wo", 0, 0)
         regroup("wo", V_COLS_WO, 1, 0)
         quantise_weight(wo_codes, wo_scales, "wo", 0, 1)
-        nc.vector.tensor_copy(out=vec_cols[:], in_=vec_ps[:, :, 0 : 2 * PASSES])
         regroup("wo", V_COLS_WO, 1, 1)
         quantise_weight(wo_codes, wo_scales, "wo", 1, 0)
         flip_attn(1)
@@ -351,20 +346,26 @@ def tile_successiveswintransfomerblock_pb_kernel(tc, attn_win, x_mid, Wo2, bo2, 
         place_attn(1)
         quantise_weight(wo_codes, wo_scales, "wo", 1, 1)
         place_attn(2)
+        vec_f32 = keep.tile([P, K_PASS], F32)
+        nc.vector.tensor_copy(out=vec_f32[:], in_=vec_rows[:])
         quantise_attn(0)
         project(0)
         spread_copy(0)
         spread_copy(1)
         xb_on_vector(0)
+        vec_ps = psum_tr.tile([P, PACK, P], F32, name="vec_ps", tag="tr")
+        for t in range(PACK):
+            nc.tensor.transpose(vec_ps[:, t, :], vec_f32[:, t::PACK], ident[:])
         for s in range(3, EARLY_ATTN):
             flip_attn(s)
             place_attn(s)
+        xb_on_vector(1)
+        quantise_attn(1)
+        nc.vector.tensor_copy(out=vec_cols[:], in_=vec_ps[:, :, 0 : 2 * PASSES])
         spread(2)
         spread(3)
         spread_copy(2)
         spread_copy(3)
-        xb_on_vector(1)
-        quantise_attn(1)
         residual(0)
         mean(0)
         project(1)
@@ -418,9 +419,9 @@ def tile_successiveswintransfomerblock_pb_kernel(tc, attn_win, x_mid, Wo2, bo2, 
                 project(k + 3)
             if k + 3 in XB_PE:
                 xb_copy(k + 3)
-            if 6 + k < TILES:
-                flip_attn(6 + k)
-                place_attn(6 + k)
+            for s in LATE_ATTN.get(k, ()):
+                flip_attn(s)
+                place_attn(s)
             if k < HALVES:
                 for g in range(PASSES):
                     quantise_weight(wl_codes, wl_scales, "wl", g, k)

@@ -30,8 +30,8 @@ FLOPS = 2 * 2 * TOKENS * D * D
 
 EARLY_ATTN = 5
 XB_PE = (3, 4, 5, 6, 7, 8)
+H_ON_SCALAR = ((7, 1), (8, 0), (8, 1))
 LATE_ATTN = {0: (6, 7), 2: (8,)}
-BL_V = (0, 6)
 EARLY_XB = 3
 V_COLS_WO = 320
 V_COLS_WL = 320
@@ -105,11 +105,12 @@ def tile_successiveswintransfomerblock_pb_kernel(tc, attn_win, x_mid, Wo2, bo2, 
             if g == 0:
                 load_rows(attn_sb, attn_src, 0, 1)
         load_rows(attn_sb, attn_src, 1, 3)
-        load_rows(attn_sb, attn_src, 3, 5)
-        load_rows(xmid_sb, xmid_src, 0, 3)
-        for g in range(PASSES):
-            load_weight("wl", wl_src, g)
-        load_rows(attn_sb, attn_src, 5, 9)
+        load_rows(xmid_sb, xmid_src, 0, 1)
+        load_weight("wl", wl_src, 0)
+        load_rows(attn_sb, attn_src, 3, 6)
+        load_rows(xmid_sb, xmid_src, 1, 3)
+        load_weight("wl", wl_src, 1)
+        load_rows(attn_sb, attn_src, 6, 9)
         load_rows(xmid_sb, xmid_src, 3, 6)
         load_rows(xmid_sb, xmid_src, 6, 9)
 
@@ -225,17 +226,28 @@ def tile_successiveswintransfomerblock_pb_kernel(tc, attn_win, x_mid, Wo2, bo2, 
                 op0=ALU.add, op1=ALU.mult,
             )
 
-        def add_bl(i):
-            for h in range(HALVES):
+        def add_bl(i, halves=range(HALVES)):
+            for h in halves:
                 cols = slice(h * N_PASS, (h + 1) * N_PASS)
                 nc.vector.tensor_tensor(
                     out=x[i][:, cols], in0=x[i][:, cols], in1=bias_all[:, D + h * N_PASS : D + (h + 1) * N_PASS], op=ALU.add
                 )
 
-        def add_bl_later(i, dtype, last_written):
+        def release_gpsimd(dtype, last_written):
             tick = small.tile([P, 1], dtype, name="tick", tag="tick")
             nc.gpsimd.tensor_copy(out=tick[:], in_=last_written)
-            nc.gpsimd.tensor_tensor(out=x[i][:], in0=x[i][:], in1=bias_all[:, D : 2 * D], op=ALU.add)
+
+        def xb_half_on_gpsimd(i, h):
+            cols = slice(h * N_PASS, (h + 1) * N_PASS)
+            if h == 0:
+                xb[i] = ahead.tile([P, D], F32, name="xb")
+            nc.gpsimd.tensor_tensor(out=xb[i][:, cols], in0=xmid_sb[:, i, cols], in1=bias_all[:, cols], op=ALU.add)
+
+        def add_bl_later(i, dtype, last_written, first=0, end=D):
+            release_gpsimd(dtype, last_written)
+            nc.gpsimd.tensor_tensor(
+                out=x[i][:, first:end], in0=x[i][:, first:end], in1=bias_all[:, D + first : D + end], op=ALU.add
+            )
 
         def square(i):
             squares = short.tile([P, D], BF16)
@@ -284,10 +296,13 @@ def tile_successiveswintransfomerblock_pb_kernel(tc, attn_win, x_mid, Wo2, bo2, 
                         out=planes[i, g][:, t, :], in_=flipped_xn[i, g][:, t, :], func=ACT.Identity, bias=bias, scale=gain
                     )
 
-        def regroup_h(i):
+        def regroup_h(i, on_scalar=False):
             for g in range(PASSES):
+                if ((i, g) in H_ON_SCALAR) != on_scalar:
+                    continue
                 h_grouped[i, g] = short.tile([P, P, PACK], BF16, align_bytes=64, name="h_grouped", tag="h_grouped%d" % g)
-                nc.vector.tensor_copy(out=h_grouped[i, g][:], in_=planes[i, g][:].rearrange("p t n -> p n t"))
+                regroup_copy = nc.scalar.copy if (i, g) in H_ON_SCALAR else nc.vector.tensor_copy
+                regroup_copy(out=h_grouped[i, g][:], in_=planes[i, g][:].rearrange("p t n -> p n t"))
 
         def quantise_h(i):
             h_codes[i] = short.tile([P, PASSES, P], U32, align_bytes=64, name="h_codes")
@@ -314,8 +329,8 @@ def tile_successiveswintransfomerblock_pb_kernel(tc, attn_win, x_mid, Wo2, bo2, 
                         stop=(g == PASSES - 1),
                     )
 
-        def finish(i):
-            for h in range(HALVES):
+        def finish(i, halves=range(HALVES)):
+            for h in halves:
                 cols = slice(h * N_PASS, (h + 1) * N_PASS)
                 nc.vector.tensor_tensor(out=x[i][:, cols], in0=acc2[i, h][:], in1=x[i][:, cols], op=ALU.add)
                 nc.sync.dma_start(out=out_rows[i * P : (i + 1) * P, cols], in_=x[i][:, cols])
@@ -331,8 +346,6 @@ def tile_successiveswintransfomerblock_pb_kernel(tc, attn_win, x_mid, Wo2, bo2, 
             nc.scalar.copy(out=bias_all[:, j * N_PASS : (j + 1) * N_PASS], in_=spread_ps[j][:])
 
         flip_attn(0)
-        spread(0)
-        spread(1)
         regroup("wo", V_COLS_WO, 0, 0)
         regroup("wo", V_COLS_WO, 0, 1)
         place_attn(0)
@@ -343,6 +356,8 @@ def tile_successiveswintransfomerblock_pb_kernel(tc, attn_win, x_mid, Wo2, bo2, 
         quantise_weight(wo_codes, wo_scales, "wo", 1, 0)
         flip_attn(1)
         flip_attn(2)
+        spread(0)
+        spread(1)
         place_attn(1)
         quantise_weight(wo_codes, wo_scales, "wo", 1, 1)
         place_attn(2)
@@ -352,30 +367,35 @@ def tile_successiveswintransfomerblock_pb_kernel(tc, attn_win, x_mid, Wo2, bo2, 
         project(0)
         spread_copy(0)
         spread_copy(1)
+        regroup("wl", V_COLS_WL, 0, 0)
+        regroup("wl", V_COLS_WL, 0, 1)
         xb_on_vector(0)
-        vec_ps = psum_tr.tile([P, PACK, P], F32, name="vec_ps", tag="tr")
+        vec_ps = psum_acc2.tile([P, PACK, P], F32, name="vec_ps", tag="acc2")
         for t in range(PACK):
             nc.tensor.transpose(vec_ps[:, t, :], vec_f32[:, t::PACK], ident[:])
         for s in range(3, EARLY_ATTN):
             flip_attn(s)
             place_attn(s)
-        xb_on_vector(1)
         quantise_attn(1)
-        nc.vector.tensor_copy(out=vec_cols[:], in_=vec_ps[:, :, 0 : 2 * PASSES])
         spread(2)
         spread(3)
-        spread_copy(2)
-        spread_copy(3)
+        release_gpsimd(U32, attn_codes[:, PASSES - 1, 2 * P - 1 : 2 * P])
+        xb_half_on_gpsimd(2, 0)
         residual(0)
         mean(0)
+        xb_on_vector(1)
         project(1)
         quantise_attn(2)
         square(0)
         scale_of(0)
-        xb_on_vector(2)
+        spread_copy(2)
+        spread_copy(3)
+        release_gpsimd(U32, attn_codes[:, PASSES - 1, 3 * P - 1 : 3 * P])
+        xb_half_on_gpsimd(2, 1)
         flip_attn(5)
         place_attn(5)
         residual(1)
+        nc.vector.tensor_copy(out=vec_cols[:], in_=vec_ps[:, :, 0 : 2 * PASSES])
         mean(1)
         project(2)
         square(1)
@@ -390,10 +410,12 @@ def tile_successiveswintransfomerblock_pb_kernel(tc, attn_win, x_mid, Wo2, bo2, 
                 normalise(last)
                 gain_and_bias(k, 0)
                 gain_and_bias(k, 1)
+                regroup_h(k, on_scalar=True)
                 flip(last)
-            if k - 1 in BL_V:
-                add_bl(k - 1)
-            elif 0 < k < last:
+                add_bl_later(k - 1, F32, xn[last, PASSES - 1][:, PACK - 1, P - 1 : P], 0, N_PASS)
+            if k < HALVES:
+                add_bl_later(0, F32, xn[k, PASSES - 1][:, PACK - 1, P - 1 : P], k * N_PASS, (k + 1) * N_PASS)
+            elif k < last - 1:
                 add_bl_later(k - 1, F32, xn[k, PASSES - 1][:, PACK - 1, P - 1 : P])
             if 1 < k < last:
                 finish(k - 2)
@@ -407,11 +429,11 @@ def tile_successiveswintransfomerblock_pb_kernel(tc, attn_win, x_mid, Wo2, bo2, 
             if k + 2 < TILES:
                 mean(k + 2)
             if k < HALVES:
-                for g in range(PASSES):
-                    regroup("wl", V_COLS_WL, g, k)
+                regroup("wl", V_COLS_WL, 1, k)
             if k != last - 1:
                 gain_and_bias(k, 0)
                 gain_and_bias(k, 1)
+                regroup_h(k, on_scalar=True)
             if k + 2 < TILES:
                 square(k + 2)
                 scale_of(k + 2)
@@ -423,17 +445,20 @@ def tile_successiveswintransfomerblock_pb_kernel(tc, attn_win, x_mid, Wo2, bo2, 
                 flip_attn(s)
                 place_attn(s)
             if k < HALVES:
-                for g in range(PASSES):
-                    quantise_weight(wl_codes, wl_scales, "wl", g, k)
+                quantise_weight(wl_codes, wl_scales, "wl", 0, k)
+                quantise_weight(wl_codes, wl_scales, "wl", 1, k)
             regroup_h(k)
             quantise_h(k)
             if k == last - 1:
                 linear(k)
-                add_bl(k)
+                add_bl(k - 1, (1,))
+                add_bl(k, (1,))
+                add_bl_later(k, F32, x[k][:, D - 1 : D], 0, N_PASS)
+                finish(k - 1)
             if k == 1:
                 linear(0)
-        add_bl_later(last, U32, h_codes[last][:, PASSES - 1, P - 1 : P])
         linear(last)
-        finish(last - 2)
+        add_bl(last, (1,))
+        add_bl_later(last, F32, x[last][:, D - 1 : D], 0, N_PASS)
         finish(last - 1)
-        finish(last)
+        finish(last, (1, 0))

@@ -30,7 +30,7 @@ FLOPS = 2 * 2 * TOKENS * D * D
 
 EARLY_ATTN = 5
 XB_PE = (3, 4, 5, 6, 7, 8)
-H_ON_SCALAR = ((7, 1), (8, 0), (8, 1))
+H_ON_SCALAR = ((5, 1), (7, 1), (8, 0), (8, 1))
 LATE_ATTN = {0: (6, 7), 2: (8,)}
 EARLY_XB = 3
 V_COLS_WO = 320
@@ -75,7 +75,6 @@ def tile_successiveswintransfomerblock_pb_kernel(tc, attn_win, x_mid, Wo2, bo2, 
         vec_rows = keep.tile([P, K_PASS], BF16)
         nc.gpsimd.memset(vec_rows[:].bitcast(F32), 0.0)
         nc.scalar.dma_start(out=bias_rows[0:1, 0:D], in_=bo2.rearrange("(o d) -> o d", o=1))
-        nc.scalar.dma_start(out=bias_rows[0:1, D : 2 * D], in_=bl.rearrange("(o d) -> o d", o=1))
         nc.scalar.dma_start(out=vec_rows[0:PASSES, :], in_=g4.rearrange("(g k) -> g k", g=PASSES))
         nc.scalar.dma_start(out=vec_rows[PASSES : 2 * PASSES, :], in_=b4.rearrange("(g k) -> g k", g=PASSES))
         ident = keep.tile([P, P], F32)
@@ -105,8 +104,9 @@ def tile_successiveswintransfomerblock_pb_kernel(tc, attn_win, x_mid, Wo2, bo2, 
             if g == 0:
                 load_rows(attn_sb, attn_src, 0, 1)
         load_rows(attn_sb, attn_src, 1, 3)
-        load_rows(xmid_sb, xmid_src, 0, 1)
         load_weight("wl", wl_src, 0)
+        load_rows(xmid_sb, xmid_src, 0, 1)
+        nc.sync.dma_start(out=bias_rows[0:1, D : 2 * D], in_=bl.rearrange("(o d) -> o d", o=1))
         load_rows(attn_sb, attn_src, 3, 6)
         load_rows(xmid_sb, xmid_src, 1, 3)
         load_weight("wl", wl_src, 1)
@@ -302,7 +302,10 @@ def tile_successiveswintransfomerblock_pb_kernel(tc, attn_win, x_mid, Wo2, bo2, 
                     continue
                 h_grouped[i, g] = short.tile([P, P, PACK], BF16, align_bytes=64, name="h_grouped", tag="h_grouped%d" % g)
                 regroup_copy = nc.scalar.copy if (i, g) in H_ON_SCALAR else nc.vector.tensor_copy
-                regroup_copy(out=h_grouped[i, g][:], in_=planes[i, g][:].rearrange("p t n -> p n t"))
+                regroup_copy(
+                    out=h_grouped[i, g][:].rearrange("p (c i) t -> p c t i", i=4),
+                    in_=planes[i, g][:].rearrange("p t (c i) -> p c t i", i=4),
+                )
 
         def quantise_h(i):
             h_codes[i] = short.tile([P, PASSES, P], U32, align_bytes=64, name="h_codes")
@@ -434,13 +437,13 @@ def tile_successiveswintransfomerblock_pb_kernel(tc, attn_win, x_mid, Wo2, bo2, 
                 gain_and_bias(k, 0)
                 gain_and_bias(k, 1)
                 regroup_h(k, on_scalar=True)
+            if k + 3 in XB_PE:
+                xb_copy(k + 3)
             if k + 2 < TILES:
                 square(k + 2)
                 scale_of(k + 2)
             if k + 3 < TILES:
                 project(k + 3)
-            if k + 3 in XB_PE:
-                xb_copy(k + 3)
             for s in LATE_ATTN.get(k, ()):
                 flip_attn(s)
                 place_attn(s)

@@ -31,6 +31,7 @@ FLOPS = 2 * 2 * TOKENS * D * D
 EARLY_ATTN = 5
 XB_PE = (3, 4, 5, 6, 7, 8)
 H_ON_SCALAR = ((5, 1), (7, 1), (8, 0), (8, 1))
+GATED = {1: 0, 2: 1, 3: 2, 4: 3, 5: 4, 6: 5, 8: 6}
 LATE_ATTN = {0: (6, 7), 2: (8,)}
 EARLY_XB = 3
 V_COLS_WO = 320
@@ -81,7 +82,8 @@ def tile_successiveswintransfomerblock_pb_kernel(tc, attn_win, x_mid, Wo2, bo2, 
         make_identity(nc, ident[:])
         ident_bf = keep.tile([P, P], BF16)
         nc.gpsimd.tensor_copy(out=ident_bf[:], in_=ident[:])
-        bias_all = keep.tile([P, 2 * D], BF16)
+        bias_all = keep.tile([P, 2 * D + 2], BF16)
+        nc.gpsimd.memset(bias_all[:, 2 * D : 2 * D + 2].bitcast(F32), 0.0)
         vec_cols = keep.tile([P, PACK, 2 * PASSES], F32)
 
         attn_sb = keep.tile([P, TILES, D], BF16)
@@ -210,7 +212,7 @@ def tile_successiveswintransfomerblock_pb_kernel(tc, attn_win, x_mid, Wo2, bo2, 
                     )
 
         def residual(i):
-            x[i] = rows_pool.tile([P, D], F32, name="x")
+            x[i] = rows_pool.tile([P, D + 1], F32, name="x")
             sums[i] = small.tile([P, HALVES], F32, name="sums")
             for h in range(HALVES):
                 cols = slice(h * N_PASS, (h + 1) * N_PASS)
@@ -220,9 +222,9 @@ def tile_successiveswintransfomerblock_pb_kernel(tc, attn_win, x_mid, Wo2, bo2, 
                 )
 
         def mean(i):
-            negmean[i] = small.tile([P, 1], F32, name="negmean")
+            negmean[i] = x[GATED[i]][:, D : D + 1] if i in GATED else small.tile([P, 1], F32, name="negmean")[:]
             nc.vector.tensor_scalar(
-                out=negmean[i][:], in0=sums[i][:, 0:1], scalar1=sums[i][:, 1:2], scalar2=-1.0 / D,
+                out=negmean[i], in0=sums[i][:, 0:1], scalar1=sums[i][:, 1:2], scalar2=-1.0 / D,
                 op0=ALU.add, op1=ALU.mult,
             )
 
@@ -249,11 +251,16 @@ def tile_successiveswintransfomerblock_pb_kernel(tc, attn_win, x_mid, Wo2, bo2, 
                 out=x[i][:, first:end], in0=x[i][:, first:end], in1=bias_all[:, D + first : D + end], op=ALU.add
             )
 
+        def add_bl_behind(i, first=0):
+            nc.gpsimd.tensor_tensor(
+                out=x[i][:, first : D + 1], in0=x[i][:, first : D + 1], in1=bias_all[:, D + first : 2 * D + 1], op=ALU.add
+            )
+
         def square(i):
             squares = short.tile([P, D], BF16)
             ssq[i] = small.tile([P, 1], F32, name="ssq")
             nc.scalar.activation(
-                out=squares[:], in_=x[i][:], func=ACT.Square, bias=negmean[i][:], scale=1.0, accum_out=ssq[i][:]
+                out=squares[:], in_=x[i][:, 0:D], func=ACT.Square, bias=negmean[i], scale=1.0, accum_out=ssq[i][:]
             )
 
         def scale_of(i):
@@ -262,7 +269,7 @@ def tile_successiveswintransfomerblock_pb_kernel(tc, attn_win, x_mid, Wo2, bo2, 
 
         def shift_of(i):
             shift[i] = small.tile([P, 1], F32, name="shift")
-            nc.scalar.activation(out=shift[i][:], in_=negmean[i][:], func=ACT.Identity, scale=rstd[i][:])
+            nc.scalar.activation(out=shift[i][:], in_=negmean[i], func=ACT.Identity, scale=rstd[i][:])
 
         def normalise(i):
             for g in range(PASSES):
@@ -271,7 +278,7 @@ def tile_successiveswintransfomerblock_pb_kernel(tc, attn_win, x_mid, Wo2, bo2, 
                 src = x[i][:, g * K_PASS : (g + 1) * K_PASS].rearrange("p (m t) -> p m t", t=PACK)
                 if i in NORM_V:
                     nc.vector.tensor_scalar(
-                        out=dst, in0=src, scalar1=negmean[i][:], scalar2=rstd[i][:], op0=ALU.add, op1=ALU.mult
+                        out=dst, in0=src, scalar1=negmean[i], scalar2=rstd[i][:], op0=ALU.add, op1=ALU.mult
                     )
                 else:
                     nc.scalar.activation(out=dst, in_=src, func=ACT.Identity, bias=shift[i][:], scale=rstd[i][:])
@@ -415,11 +422,13 @@ def tile_successiveswintransfomerblock_pb_kernel(tc, attn_win, x_mid, Wo2, bo2, 
                 gain_and_bias(k, 1)
                 regroup_h(k, on_scalar=True)
                 flip(last)
-                add_bl_later(k - 1, F32, xn[last, PASSES - 1][:, PACK - 1, P - 1 : P], 0, N_PASS)
-            if k < HALVES:
-                add_bl_later(0, F32, xn[k, PASSES - 1][:, PACK - 1, P - 1 : P], k * N_PASS, (k + 1) * N_PASS)
+                add_bl_behind(k - 1, N_PASS)
+            if k == 0:
+                add_bl_later(0, F32, xn[0, PASSES - 1][:, PACK - 1, P - 1 : P], 0, N_PASS)
+            elif k == 1:
+                add_bl_behind(0, N_PASS)
             elif k < last - 1:
-                add_bl_later(k - 1, F32, xn[k, PASSES - 1][:, PACK - 1, P - 1 : P])
+                add_bl_behind(k - 1)
             if 1 < k < last:
                 finish(k - 2)
                 linear(k - 1)
@@ -454,7 +463,7 @@ def tile_successiveswintransfomerblock_pb_kernel(tc, attn_win, x_mid, Wo2, bo2, 
             quantise_h(k)
             if k == last - 1:
                 linear(k)
-                add_bl(k - 1, (1,))
+                add_bl(k - 1, (0,))
                 add_bl(k, (1,))
                 add_bl_later(k, F32, x[k][:, D - 1 : D], 0, N_PASS)
                 finish(k - 1)

@@ -473,4 +473,8 @@ def tile_successiveswintransfomerblock_pb_kernel(tc, attn_win, x_mid, Wo2, bo2, 
         add_bl(last, (1,))
         add_bl_later(last, F32, x[last][:, D - 1 : D], 0, N_PASS)
         finish(last - 1)
-        finish(last, (1, 0))
+        finish(last, (1,))
+        for first in (0, N_PASS // 2):
+            cols = slice(first, first + N_PASS // 2)
+            nc.vector.tensor_tensor(out=x[last][:, cols], in0=acc2[last, 0][:, cols], in1=x[last][:, cols], op=ALU.add)
+            nc.sync.dma_start(out=out_rows[last * P : TOKENS, cols], in_=x[last][:, cols])

from contextlib import ExitStack

import concourse.mybir as mybir
from concourse.masks import make_identity

F32 = mybir.dt.float32
BF16 = mybir.dt.bfloat16
U32 = mybir.dt.uint32
U8 = mybir.dt.uint8
FP8X4 = mybir.dt.float8_e4m3fn_x4
ALU = mybir.AluOpType
ACT = mybir.ActivationFunctionType

P = 128
D = 1024
PACK = 4
K_PASS = P * PACK
PASSES = D // K_PASS
N_PASS = 512
HALVES = D // N_PASS
IMAGES = 2
SIDE = 24
WS = 8
WN = SIDE // WS
SHIFT = WS // 2
TOKENS = IMAGES * SIDE * SIDE
TILES = TOKENS // P
LN_EPS = 1e-5
FLOPS = 2 * 2 * TOKENS * D * D

EARLY_ATTN = 5
XB_PE = (3, 4, 5, 6, 7, 8)
H_ON_SCALAR = ((5, 1), (7, 1), (8, 0), (8, 1))
GATED = {1: 0, 2: 1, 3: 2, 4: 3, 5: 4, 6: 5, 8: 6}
LATE_ATTN = {0: (6, 7), 2: (8,)}
EARLY_XB = 3
V_COLS_WO = 320
V_COLS_WL = 320
NORM_V = tuple(range(TILES))


def rolled_runs(w):
    start = WS * w - SHIFT
    if start < 0:
        return [(0, SHIFT, start + SIDE), (SHIFT, WS - SHIFT, 0)]
    return [(0, WS, start)]


def tile_successiveswintransfomerblock_pb_kernel(tc, attn_win, x_mid, Wo2, bo2, g4, b4, Wl, bl, out):
    nc = tc.nc
    attn_rows = attn_win.flatten_outer_dims()
    xmid_rows = x_mid.flatten_outer_dims()
    out_rows = out.flatten_outer_dims()

    with ExitStack() as ctx:
        keep = ctx.enter_context(tc.tile_pool(name="keep", bufs=1))
        stage = ctx.enter_context(tc.tile_pool(name="stage", bufs=4))
        ahead = ctx.enter_context(tc.tile_pool(name="ahead", bufs=4))
        rows_pool = ctx.enter_context(tc.tile_pool(name="rows_pool", bufs=7))
        short = ctx.enter_context(tc.tile_pool(name="short", bufs=3))
        small = ctx.enter_context(tc.tile_pool(name="small", bufs=8))
        psum_acc1 = ctx.enter_context(tc.psum_pool(name="psum_acc1", bufs=2))
        psum_mix = ctx.enter_context(tc.psum_pool(name="psum_mix", bufs=2))
        psum_acc2 = ctx.enter_context(tc.psum_pool(name="psum_acc2", bufs=2))
        psum_tr = ctx.enter_context(tc.psum_pool(name="psum_tr", bufs=2))
        ctx.enter_context(tc.manual_schedule())

        ones = keep.tile([P, P], BF16)
        nc.vector.memset(ones[:], 1.0)
        eps = keep.tile([P, 1], F32)
        nc.vector.memset(eps[:], LN_EPS)
        warm = keep.tile([P, 1], F32)
        nc.scalar.activation(out=warm[:], in_=eps[:], func=ACT.Abs_reciprocal_sqrt)
        bias_rows = keep.tile([P, 2 * D], BF16)
        nc.vector.memset(bias_rows[:].bitcast(F32), 0.0)
        vec_rows = keep.tile([P, K_PASS], BF16)
        nc.gpsimd.memset(vec_rows[:].bitcast(F32), 0.0)
        nc.scalar.dma_start(out=bias_rows[0:1, 0:D], in_=bo2.rearrange("(o d) -> o d", o=1))
        nc.scalar.dma_start(out=vec_rows[0:PASSES, :], in_=g4.rearrange("(g k) -> g k", g=PASSES))
        nc.scalar.dma_start(out=vec_rows[PASSES : 2 * PASSES, :], in_=b4.rearrange("(g k) -> g k", g=PASSES))
        ident = keep.tile([P, P], F32)
        make_identity(nc, ident[:])
        ident_bf = keep.tile([P, P], BF16)
        nc.gpsimd.tensor_copy(out=ident_bf[:], in_=ident[:])
        bias_all = keep.tile([P, 2 * D + 2], BF16)
        nc.gpsimd.memset(bias_all[:, 2 * D : 2 * D + 2].bitcast(F32), 0.0)
        vec_cols = keep.tile([P, PACK, 2 * PASSES], F32)

        attn_sb = keep.tile([P, TILES, D], BF16)
        attn_src = attn_rows.rearrange("(s q) d -> q s d", q=P)
        xmid_sb = keep.tile([P, TILES, D], BF16)
        xmid_src = xmid_rows.rearrange("(s q) d -> q s d", q=P)
        wo_src = Wo2.rearrange("(g p t) n -> p g t n", p=P, t=PACK)
        wl_src = Wl.rearrange("(g p t) n -> p g t n", p=P, t=PACK)
        raw = {}

        def load_weight(name, src, g):
            raw[name, g] = keep.tile([P, PACK, D], BF16, name="raw", tag="raw_%s_%d" % (name, g))
            nc.sync.dma_start(out=raw[name, g][:], in_=src[:, g, :, :])

        def load_rows(dst, src, first, last):
            nc.sync.dma_start(out=dst[:, first:last, :], in_=src[:, first:last, :])

        for g in range(PASSES):
            load_weight("wo", wo_src, g)
            if g == 0:
                load_rows(attn_sb, attn_src, 0, 1)
        load_rows(attn_sb, attn_src, 1, 3)
        load_weight("wl", wl_src, 0)
        load_rows(xmid_sb, xmid_src, 0, 1)
        nc.sync.dma_start(out=bias_rows[0:1, D : 2 * D], in_=bl.rearrange("(o d) -> o d", o=1))
        load_rows(attn_sb, attn_src, 3, 6)
        load_rows(xmid_sb, xmid_src, 1, 3)
        load_weight("wl", wl_src, 1)
        load_rows(attn_sb, attn_src, 6, 9)
        load_rows(xmid_sb, xmid_src, 3, 6)
        load_rows(xmid_sb, xmid_src, 6, 9)

        wo_codes = keep.tile([P, PASSES, D], U32, align_bytes=64)
        wo_scales = keep.tile([P, PASSES, D], U8, align_bytes=64)
        wl_codes = keep.tile([P, PASSES, D], U32, align_bytes=64)
        wl_scales = keep.tile([P, PASSES, D], U8, align_bytes=64)
        attn_grouped = keep.tile([P, PASSES, TOKENS, PACK], BF16, align_bytes=64)
        attn_codes = keep.tile([P, PASSES, TOKENS], U32, align_bytes=64)
        attn_scales = keep.tile([P, PASSES, TOKENS], U8, align_bytes=64)
        by_patch = attn_grouped[:].bitcast(F32).rearrange("p g (b r c) u -> p g b r c u", r=SIDE, c=SIDE)

        grouped = {}

        def regroup(name, v_cols, g, h):
            grouped[name, g, h] = stage.tile([P, N_PASS, PACK], BF16, align_bytes=64, name="grouped")
            dst = grouped[name, g, h]
            src = raw[name, g][:, :, h * N_PASS : (h + 1) * N_PASS]
            for engine_copy, cols in ((nc.vector.tensor_copy, slice(0, v_cols)), (nc.scalar.copy, slice(v_cols, N_PASS))):
                engine_copy(
                    out=dst[:, cols, :].rearrange("p (c i) t -> p c t i", i=4),
                    in_=src[:, :, cols].rearrange("p t (c i) -> p c t i", i=4),
                )

        def quantise_weight(codes, scales, name, g, h):
            cols = slice(h * N_PASS, (h + 1) * N_PASS)
            nc.vector.quantize_mx(
                out=codes[:, g, cols].bitcast(FP8X4), scales=scales[:, g, cols],
                in_=grouped[name, g, h][:].rearrange("p n t -> p (n t)"),
            )

        flipped_attn = {}

        def flip_attn(s):
            pool, tag = (psum_acc2, "acc2") if s in (1, 2, 4, 6, 7) else (psum_mix, "mix")
            flipped_attn[s] = pool.tile([P, PASSES * 2, P], F32, name="flipped_attn", tag=tag)
            for c in range(PASSES * 2):
                g, u = divmod(c, 2)
                words = attn_sb[:, s, :].bitcast(F32)[:, 2 * P * g + u : 2 * P * (g + 1) : 2]
                nc.tensor.transpose(flipped_attn[s][:, c, :], words, ident[:])

        def place_attn(s):
            by_window = flipped_attn[s][:].rearrange("p c (w i j) -> p c w i j", i=WS, j=WS)
            for w in range(2):
                image, in_image = divmod(2 * s + w, WN * WN)
                wr, wc = divmod(in_image, WN)
                for i0, n_rows, r0 in rolled_runs(wr):
                    for j0, n_cols, c0 in rolled_runs(wc):
                        for g in range(PASSES):
                            src = by_window[:, 2 * g : 2 * g + 2, w, i0 : i0 + n_rows, j0 : j0 + n_cols]
                            dst = by_patch[:, g, image, r0 : r0 + n_rows, c0 : c0 + n_cols, :]
                            nc.scalar.copy(out=dst, in_=src.rearrange("p u i j -> p i j u"))

        def quantise_attn(i):
            toks = slice(i * P, (i + 1) * P)
            for g in range(PASSES):
                nc.vector.quantize_mx(
                    out=attn_codes[:, g, toks].bitcast(FP8X4),
                    scales=attn_scales[:, g, toks],
                    in_=attn_grouped[:, g, toks, :].rearrange("p n t -> p (n t)"),
                )

        xb, xb_ps, acc1, x, sums, negmean, ssq, rstd, shift, xn, flipped_xn, planes, h_grouped, h_codes, h_scales, acc2 = (
            {}, {}, {}, {}, {}, {}, {}, {}, {}, {}, {}, {}, {}, {}, {}, {},
        )

        def xb_on_vector(i):
            xb[i] = ahead.tile([P, D], F32, name="xb")
            nc.vector.tensor_tensor(out=xb[i][:], in0=xmid_sb[:, i, :], in1=bias_all[:, 0:D], op=ALU.add)

        def xb_on_tensor(i):
            for h in range(HALVES):
                cols = slice(h * N_PASS, (h + 1) * N_PASS)
                xb_ps[i, h] = psum_mix.tile([P, N_PASS], F32, name="xb_ps", tag="mix")
                nc.tensor.matmul(out=xb_ps[i, h][:], lhsT=ones[:], rhs=bias_rows[:, cols], start=True, stop=False)
                nc.tensor.matmul(out=xb_ps[i, h][:], lhsT=ident_bf[:], rhs=xmid_sb[:, i, cols], start=False, stop=True)

        def xb_copy(i):
            xb[i] = ahead.tile([P, D], F32, name="xb")
            for h in range(HALVES):
                nc.scalar.copy(out=xb[i][:, h * N_PASS : (h + 1) * N_PASS], in_=xb_ps[i, h][:])

        def project(i):
            toks = slice(i * P, (i + 1) * P)
            for h in range(HALVES):
                cols = slice(h * N_PASS, (h + 1) * N_PASS)
                acc1[i, h] = psum_acc1.tile([P, N_PASS], F32, name="acc1", tag="acc1")
                for g in range(PASSES):
                    nc.tensor.matmul_mx(
                        out=acc1[i, h][:],
                        lhsT=attn_codes[:, g, toks].bitcast(FP8X4),
                        lhsT_scale=attn_scales[:, g, toks],
                        rhs=wo_codes[:, g, cols].bitcast(FP8X4),
                        rhs_scale=wo_scales[:, g, cols],
                        start=(g == 0),
                        stop=(g == PASSES - 1),
                    )

        def residual(i):
            x[i] = rows_pool.tile([P, D + 1], F32, name="x")
            sums[i] = small.tile([P, HALVES], F32, name="sums")
            for h in range(HALVES):
                cols = slice(h * N_PASS, (h + 1) * N_PASS)
                nc.vector.scalar_tensor_tensor(
                    out=x[i][:, cols], in0=acc1[i, h][:], scalar=1.0, in1=xb[i][:, cols],
                    op0=ALU.mult, op1=ALU.add, accum_out=sums[i][:, h : h + 1],
                )

        def mean(i):
            negmean[i] = x[GATED[i]][:, D : D + 1] if i in GATED else small.tile([P, 1], F32, name="negmean")[:]
            nc.vector.tensor_scalar(
                out=negmean[i], in0=sums[i][:, 0:1], scalar1=sums[i][:, 1:2], scalar2=-1.0 / D,
                op0=ALU.add, op1=ALU.mult,
            )

        def add_bl(i, halves=range(HALVES)):
            for h in halves:
                cols = slice(h * N_PASS, (h + 1) * N_PASS)
                nc.vector.tensor_tensor(
                    out=x[i][:, cols], in0=x[i][:, cols], in1=bias_all[:, D + h * N_PASS : D + (h + 1) * N_PASS], op=ALU.add
                )

        def release_gpsimd(dtype, last_written):
            tick = small.tile([P, 1], dtype, name="tick", tag="tick")
            nc.gpsimd.tensor_copy(out=tick[:], in_=last_written)

        def xb_half_on_gpsimd(i, h):
            cols = slice(h * N_PASS, (h + 1) * N_PASS)
            if h == 0:
                xb[i] = ahead.tile([P, D], F32, name="xb")
            nc.gpsimd.tensor_tensor(out=xb[i][:, cols], in0=xmid_sb[:, i, cols], in1=bias_all[:, cols], op=ALU.add)

        def add_bl_later(i, dtype, last_written, first=0, end=D):
            release_gpsimd(dtype, last_written)
            nc.gpsimd.tensor_tensor(
                out=x[i][:, first:end], in0=x[i][:, first:end], in1=bias_all[:, D + first : D + end], op=ALU.add
            )

        def add_bl_behind(i, first=0):
            nc.gpsimd.tensor_tensor(
                out=x[i][:, first : D + 1], in0=x[i][:, first : D + 1], in1=bias_all[:, D + first : 2 * D + 1], op=ALU.add
            )

        def square(i):
            squares = short.tile([P, D], BF16)
            ssq[i] = small.tile([P, 1], F32, name="ssq")
            nc.scalar.activation(
                out=squares[:], in_=x[i][:, 0:D], func=ACT.Square, bias=negmean[i], scale=1.0, accum_out=ssq[i][:]
            )

        def scale_of(i):
            rstd[i] = small.tile([P, 1], F32, name="rstd")
            nc.scalar.activation(out=rstd[i][:], in_=ssq[i][:], func=ACT.Abs_reciprocal_sqrt, bias=eps[:], scale=1.0 / D)

        def shift_of(i):
            shift[i] = small.tile([P, 1], F32, name="shift")
            nc.scalar.activation(out=shift[i][:], in_=negmean[i], func=ACT.Identity, scale=rstd[i][:])

        def normalise(i):
            for g in range(PASSES):
                xn[i, g] = short.tile([P, PACK, P], F32, name="xn", tag="xn%d" % g)
                dst = xn[i, g][:].rearrange("p t m -> p m t")
                src = x[i][:, g * K_PASS : (g + 1) * K_PASS].rearrange("p (m t) -> p m t", t=PACK)
                if i in NORM_V:
                    nc.vector.tensor_scalar(
                        out=dst, in0=src, scalar1=negmean[i], scalar2=rstd[i][:], op0=ALU.add, op1=ALU.mult
                    )
                else:
                    nc.scalar.activation(out=dst, in_=src, func=ACT.Identity, bias=shift[i][:], scale=rstd[i][:])

        def flip(i):
            for g in range(PASSES):
                flipped_xn[i, g] = psum_tr.tile([P, PACK, P], F32, name="flipped_xn", tag="tr")
                for t in range(PACK):
                    nc.tensor.transpose(flipped_xn[i, g][:, t, :], xn[i, g][:, t, :], ident[:])

        def gain_and_bias(i, g, on_vector=False):
            planes[i, g] = short.tile([P, PACK, P], BF16, name="planes", tag="planes%d" % g)
            for t in range(PACK):
                gain, bias = vec_cols[:, t, g : g + 1], vec_cols[:, t, PASSES + g : PASSES + g + 1]
                if on_vector:
                    nc.vector.tensor_scalar(
                        out=planes[i, g][:, t, :], in0=flipped_xn[i, g][:, t, :], scalar1=gain, scalar2=bias,
                        op0=ALU.mult, op1=ALU.add,
                    )
                else:
                    nc.scalar.activation(
                        out=planes[i, g][:, t, :], in_=flipped_xn[i, g][:, t, :], func=ACT.Identity, bias=bias, scale=gain
                    )

        def regroup_h(i, on_scalar=False):
            for g in range(PASSES):
                if ((i, g) in H_ON_SCALAR) != on_scalar:
                    continue
                h_grouped[i, g] = short.tile([P, P, PACK], BF16, align_bytes=64, name="h_grouped", tag="h_grouped%d" % g)
                regroup_copy = nc.scalar.copy if (i, g) in H_ON_SCALAR else nc.vector.tensor_copy
                regroup_copy(
                    out=h_grouped[i, g][:].rearrange("p (c i) t -> p c t i", i=4),
                    in_=planes[i, g][:].rearrange("p t (c i) -> p c t i", i=4),
                )

        def quantise_h(i):
            h_codes[i] = short.tile([P, PASSES, P], U32, align_bytes=64, name="h_codes")
            h_scales[i] = short.tile([P, PASSES, P], U8, align_bytes=64, name="h_scales")
            for g in range(PASSES):
                nc.vector.quantize_mx(
                    out=h_codes[i][:, g, :].bitcast(FP8X4), scales=h_scales[i][:, g, :],
                    in_=h_grouped[i, g][:].rearrange("p n t -> p (n t)"),
                )

        def linear(i):
            for h in range(HALVES):
                cols = slice(h * N_PASS, (h + 1) * N_PASS)
                pool, tag = {TILES - 2: (psum_mix, "mix"), TILES - 1: (psum_acc1, "acc1")}.get(i, (psum_acc2, "acc2"))
                acc2[i, h] = pool.tile([P, N_PASS], F32, name="acc2", tag=tag)
                for g in range(PASSES):
                    nc.tensor.matmul_mx(
                        out=acc2[i, h][:],
                        lhsT=h_codes[i][:, g, :].bitcast(FP8X4),
                        lhsT_scale=h_scales[i][:, g, :],
                        rhs=wl_codes[:, g, cols].bitcast(FP8X4),
                        rhs_scale=wl_scales[:, g, cols],
                        start=(g == 0),
                        stop=(g == PASSES - 1),
                    )

        def finish(i, halves=range(HALVES)):
            for h in halves:
                cols = slice(h * N_PASS, (h + 1) * N_PASS)
                nc.vector.tensor_tensor(out=x[i][:, cols], in0=acc2[i, h][:], in1=x[i][:, cols], op=ALU.add)
                nc.sync.dma_start(out=out_rows[i * P : (i + 1) * P, cols], in_=x[i][:, cols])

        spread_ps = {}

        def spread(j):
            cols = slice(j * N_PASS, (j + 1) * N_PASS)
            spread_ps[j] = psum_tr.tile([P, N_PASS], F32, name="spread_ps", tag="tr")
            nc.tensor.matmul(out=spread_ps[j][:], lhsT=ones[:], rhs=bias_rows[:, cols], start=True, stop=True)

        def spread_copy(j):
            nc.scalar.copy(out=bias_all[:, j * N_PASS : (j + 1) * N_PASS], in_=spread_ps[j][:])

        flip_attn(0)
        regroup("wo", V_COLS_WO, 0, 0)
        regroup("wo", V_COLS_WO, 0, 1)
        place_attn(0)
        quantise_weight(wo_codes, wo_scales, "wo", 0, 0)
        regroup("wo", V_COLS_WO, 1, 0)
        quantise_weight(wo_codes, wo_scales, "wo", 0, 1)
        regroup("wo", V_COLS_WO, 1, 1)
        quantise_weight(wo_codes, wo_scales, "wo", 1, 0)
        flip_attn(1)
        flip_attn(2)
        spread(0)
        spread(1)
        place_attn(1)
        quantise_weight(wo_codes, wo_scales, "wo", 1, 1)
        place_attn(2)
        vec_f32 = keep.tile([P, K_PASS], F32)
        nc.vector.tensor_copy(out=vec_f32[:], in_=vec_rows[:])
        quantise_attn(0)
        project(0)
        spread_copy(0)
        spread_copy(1)
        regroup("wl", V_COLS_WL, 0, 0)
        regroup("wl", V_COLS_WL, 0, 1)
        xb_on_vector(0)
        vec_ps = psum_acc2.tile([P, PACK, P], F32, name="vec_ps", tag="acc2")
        for t in range(PACK):
            nc.tensor.transpose(vec_ps[:, t, :], vec_f32[:, t::PACK], ident[:])
        for s in range(3, EARLY_ATTN):
            flip_attn(s)
            place_attn(s)
        quantise_attn(1)
        spread(2)
        spread(3)
        release_gpsimd(U32, attn_codes[:, PASSES - 1, 2 * P - 1 : 2 * P])
        xb_half_on_gpsimd(2, 0)
        residual(0)
        mean(0)
        xb_on_vector(1)
        project(1)
        quantise_attn(2)
        square(0)
        scale_of(0)
        spread_copy(2)
        spread_copy(3)
        release_gpsimd(U32, attn_codes[:, PASSES - 1, 3 * P - 1 : 3 * P])
        xb_half_on_gpsimd(2, 1)
        flip_attn(5)
        place_attn(5)
        residual(1)
        nc.vector.tensor_copy(out=vec_cols[:], in_=vec_ps[:, :, 0 : 2 * PASSES])
        mean(1)
        project(2)
        square(1)
        scale_of(1)

        last = TILES - 1
        for k in range(TILES):
            if k < last:
                normalise(k)
                flip(k)
            if k == last - 1:
                normalise(last)
                gain_and_bias(k, 0)
                gain_and_bias(k, 1)
                regroup_h(k, on_scalar=True)
                flip(last)
                add_bl_behind(k - 1, N_PASS)
            if k == 0:
                add_bl_later(0, F32, xn[0, PASSES - 1][:, PACK - 1, P - 1 : P], 0, N_PASS)
            elif k == 1:
                add_bl_behind(0, N_PASS)
            elif k < last - 1:
                add_bl_behind(k - 1)
            if 1 < k < last:
                finish(k - 2)
                linear(k - 1)
            if k + 3 in XB_PE:
                xb_on_tensor(k + 3)
            if k + 2 < TILES:
                residual(k + 2)
            if k + 3 < TILES:
                quantise_attn(k + 3)
            if k + 2 < TILES:
                mean(k + 2)
            if k < HALVES:
                regroup("wl", V_COLS_WL, 1, k)
            if k != last - 1:
                gain_and_bias(k, 0)
                gain_and_bias(k, 1)
                regroup_h(k, on_scalar=True)
            if k + 3 in XB_PE:
                xb_copy(k + 3)
            if k + 2 < TILES:
                square(k + 2)
                scale_of(k + 2)
            if k + 3 < TILES:
                project(k + 3)
            for s in LATE_ATTN.get(k, ()):
                flip_attn(s)
                place_attn(s)
            if k < HALVES:
                quantise_weight(wl_codes, wl_scales, "wl", 0, k)
                quantise_weight(wl_codes, wl_scales, "wl", 1, k)
            regroup_h(k)
            quantise_h(k)
            if k == last - 1:
                linear(k)
                add_bl(k - 1, (0,))
                add_bl(k, (1,))
                add_bl_later(k, F32, x[k][:, D - 1 : D], 0, N_PASS)
                finish(k - 1)
            if k == 1:
                linear(0)
        linear(last)
        add_bl(last, (1,))
        add_bl_later(last, F32, x[last][:, D - 1 : D], 0, N_PASS)
        finish(last - 1)
        finish(last, (1,))
        for first in (0, N_PASS // 2):
            cols = slice(first, first + N_PASS // 2)
            nc.vector.tensor_tensor(out=x[last][:, cols], in0=acc2[last, 0][:, cols], in1=x[last][:, cols], op=ALU.add)
            nc.sync.dma_start(out=out_rows[last * P : TOKENS, cols], in_=x[last][:, cols])
